import numpy as np
import ml_dtypes


def mxq(x, axis, fmt="e4m3"):
    dtype, down = {"e4m3": (ml_dtypes.float8_e4m3fn, 7), "e5m2": (ml_dtypes.float8_e5m2, 14)}[fmt]
    v = np.moveaxis(np.asarray(x, np.float32).astype(ml_dtypes.bfloat16).astype(np.float64), axis, -1)
    blocks = v.reshape(v.shape[:-1] + (-1, 32))
    amax = np.abs(blocks).max(-1, keepdims=True)
    byte = np.maximum(np.where(amax > 0, np.frexp(amax)[1] - 1 + 127, 0) - down, 1)
    scale = np.exp2(byte - 127.0)
    codes = (blocks / scale).astype(np.float32).astype(dtype).astype(np.float64)
    return np.moveaxis((codes * scale).reshape(v.shape), -1, axis)


WIDE = False


def mx_kscale(k):
    if not WIDE:
        return np.ones(k)
    levels = np.array([10, -10, 5, -5, 0])
    a = np.random.permutation(np.resize(levels, k // 512 * 4)).reshape(k // 512, 4)
    idx = np.arange(k)
    return np.exp2(a[idx // 512, idx % 128 // 32])


BF16 = ml_dtypes.bfloat16


def bf(x):
    return np.asarray(x, np.float32).astype(BF16)


def f64(x):
    return np.asarray(x).astype(np.float64)


S, B, D, H, DH = 512, 2, 1024, 8, 128


def setup_inputs():
    s = mx_kscale(D)
    return {"q": bf(np.random.standard_normal((B, H, S, DH))),
            "k": bf(np.random.standard_normal((B, H, S, DH))),
            "x": bf(np.random.standard_normal((S, B, D)) * s),
            "wv": bf(np.random.standard_normal((H, DH, D)) * 3.0 / np.sqrt(D) / s),
            "mask": bf(np.random.uniform(size=(B, S)) > 0.2)}


def reference(q, k, x, wv, mask):
    v = mxq(f64(x), 2, "e4m3").reshape(S * B, D) @ mxq(f64(wv), 2, "e4m3").reshape(H * DH, D).T
    v = v.reshape(S, B, H, DH).transpose(1, 2, 0, 3)
    sc = f64(q) @ f64(k).transpose(0, 1, 3, 2)
    a = np.tanh(sc / np.sqrt(DH)) - 10000.0 * (1.0 - f64(mask))[:, None, None, :]
    e = np.exp(a - a.max(-1, keepdims=True))
    o = (mxq(e, 3, "e4m3") @ mxq(v, 2, "e4m3")) / e.sum(-1, keepdims=True)
    return o.transpose(2, 0, 1, 3).reshape(S, B, H * DH)

@@ -1,0 +1,277 @@
+import math
+from contextlib import ExitStack
+
+import concourse.mybir as mybir
+from concourse.masks import make_identity
+
+F32 = mybir.dt.float32
+BF16 = mybir.dt.bfloat16
+U32 = mybir.dt.uint32
+U8 = mybir.dt.uint8
+FP8X4 = mybir.dt.float8_e4m3fn_x4
+ACT = mybir.ActivationFunctionType
+ALU = mybir.AluOpType
+AXIS = mybir.AxisListType
+
+P = 128
+S, B, D, H, DH = 512, 2, 1024, 8, 128
+HEADS = B * H
+TILES = S // P
+PASSES = D // 512
+FLOPS = 2 * (S * B) * (H * DH) * D + 2 * 2 * HEADS * S * S * DH
+
+TURN_QK = 0
+MULTIPLY_QK = 1
+TANH = 2
+PROJECT_V = 3
+ROW_MAX = 4
+EXP = 5
+ATTEND = 6
+FIRST_ROWS_STEP = 2
+ROWS_PER_STEP = 4
+
+
+def tile_attention_pa_kernel(tc, q, k, x, wv, mask, out):
+    nc = tc.nc
+    with ExitStack() as stack:
+        keep = stack.enter_context(tc.tile_pool(name="keep", bufs=1))
+        pair = stack.enter_context(tc.tile_pool(name="pair", bufs=2))
+        trio = stack.enter_context(tc.tile_pool(name="trio", bufs=3))
+        four = stack.enter_context(tc.tile_pool(name="four", bufs=4))
+        score_banks = stack.enter_context(tc.psum_pool(name="score_banks", bufs=4))
+        qk_banks = stack.enter_context(tc.psum_pool(name="qk_banks", bufs=1))
+        word_banks = stack.enter_context(tc.psum_pool(name="word_banks", bufs=2))
+        product_banks = stack.enter_context(tc.psum_pool(name="product_banks", bufs=1))
+        stack.enter_context(tc.manual_schedule())
+
+        ident_bf16 = keep.tile([P, P], BF16)
+        make_identity(nc, ident_bf16[:])
+        ident_f32 = keep.tile([P, P], F32)
+        make_identity(nc, ident_f32[:])
+
+        q_sb = keep.tile([P, HEADS, TILES, DH], BF16)
+        k_sb = keep.tile([P, HEADS, TILES, DH], BF16)
+        q_rows = q.rearrange("b h (p n) d -> p (b h) n d", n=TILES)
+        k_rows = k.rearrange("b h (n p) d -> p (b h) n d", p=P)
+        x_sb = keep.tile([P, 2, 2 * B * D], BF16)
+        x_rows = x.rearrange("(u p e) b d -> p u (e b d)", u=2, e=2)
+        wv_sb = keep.tile([P, H, D], BF16)
+        wv_rows = wv.rearrange("h c d -> c h d")
+        mask_sb = keep.tile([P, B * S], BF16)
+
+        def load_qk(two):
+            heads = slice(2 * two, 2 * two + 2)
+            nc.sync.dma_start(out=q_sb[:, heads], in_=q_rows[:, heads])
+            nc.sync.dma_start(out=k_sb[:, heads], in_=k_rows[:, heads])
+
+        load_qk(0)
+        nc.sync.dma_start(out=mask_sb[:], in_=mask.rearrange("b t -> (b t)").partition_broadcast(P))
+        load_qk(1)
+        nc.sync.dma_start(out=x_sb[:, 0], in_=x_rows[:, 0])
+        nc.sync.dma_start(out=x_sb[:, 1], in_=x_rows[:, 1])
+        nc.sync.dma_start(out=wv_sb[:, 0:4], in_=wv_rows[:, 0:4])
+        load_qk(2)
+        nc.sync.dma_start(out=wv_sb[:, 4:8], in_=wv_rows[:, 4:8])
+        for two in range(3, HEADS // 2):
+            load_qk(two)
+
+        penalty = keep.tile([P, B, S], F32)
+        nc.vector.tensor_scalar(
+            out=penalty[:].rearrange("p b t -> p (b t)"),
+            in0=mask_sb[:],
+            scalar1=-10000.0,
+            scalar2=10000.0,
+            op0=ALU.mult,
+            op1=ALU.add,
+        )
+
+        x_words = x_sb[:].bitcast(F32).rearrange("p u (e b w) -> p u e b w", e=2, b=B)
+        wv_words = wv_sb[:].bitcast(F32)
+        x_codes = keep.tile([P, B * TILES, PASSES, P], U32, align_bytes=64)
+        x_scales = keep.tile([P, B * TILES, PASSES, P], U8, align_bytes=64)
+        wv_codes = keep.tile([P, H, PASSES, DH], U32, align_bytes=64)
+        wv_scales = keep.tile([P, H, PASSES, DH], U8, align_bytes=64)
+        v_codes = keep.tile([P, HEADS, DH], U32, align_bytes=64)
+        v_scales = keep.tile([P, HEADS, DH], U8, align_bytes=64)
+
+        row_blocks = []
+        for t in range(TILES):
+            row_blocks.append((x_words[:, t // 2, t % 2, 0, :], x_codes[:, t], x_scales[:, t]))
+        for h in range(H):
+            row_blocks.append((wv_words[:, h, :], wv_codes[:, h], wv_scales[:, h]))
+        for t in range(TILES):
+            row_blocks.append(
+                (x_words[:, t // 2, t % 2, 1, :], x_codes[:, TILES + t], x_scales[:, TILES + t])
+            )
+
+        def quantise_rows(rows_words, codes, scales):
+            turned = word_banks.tile([P, 2, PASSES, P], F32, tag="turned")
+            for g in range(PASSES):
+                for u in range(2):
+                    first = 256 * g + 128 * u
+                    nc.tensor.transpose(turned[:, u, g, :], rows_words[:, first : first + P], ident_f32[:])
+            grouped = trio.tile([P, PASSES * P * 4], BF16, align_bytes=64)
+            nc.scalar.copy(
+                out=grouped[:].bitcast(F32).rearrange("p (g c u) -> p g c u", g=PASSES, u=2),
+                in_=turned[:].rearrange("p u g c -> p g c u"),
+            )
+            nc.vector.quantize_mx(
+                out=codes.rearrange("p g c -> p (g c)").bitcast(FP8X4),
+                scales=scales.rearrange("p g c -> p (g c)"),
+                in_=grouped[:],
+            )
+
+        qk_turned, score, minus_a, minus_max, row_sum = {}, {}, {}, {}, {}
+        e_turned, v_bank, v_grouped = {}, {}, {}
+
+        def turn_qk(s):
+            bank = qk_banks.tile([P, 2 * TILES, P], BF16)
+            for n in range(TILES):
+                nc.tensor.transpose(bank[:, n, :], q_sb[:, s, n, :], ident_bf16[:])
+            for n in range(TILES):
+                nc.tensor.transpose(bank[:, TILES + n, :], k_sb[:, s, n, :], ident_bf16[:])
+            qk_turned[s] = pair.tile([P, 2 * TILES, P], BF16, name="qk_turned")
+            nc.vector.tensor_copy(out=qk_turned[s][:], in_=bank[:])
+
+        def multiply_qk(s):
+            for n in range(TILES):
+                score[s, n] = score_banks.tile([P, S], F32, name="score")
+                nc.tensor.matmul(
+                    out=score[s, n][:],
+                    lhsT=qk_turned[s][:, n, :],
+                    rhs=qk_turned[s][:, TILES : 2 * TILES, :].rearrange("p n t -> p (n t)"),
+                    start=True,
+                    stop=True,
+                )
+
+        def tanh_and_mask(s):
+            minus_a[s] = four.tile([P, TILES, S], F32, name="minus_a")
+            for n in range(TILES):
+                nc.scalar.activation(
+                    out=minus_a[s][:, n, :], in_=score[s, n][:], func=ACT.Tanh, scale=1.0 / math.sqrt(DH)
+                )
+            nc.gpsimd.tensor_tensor(
+                out=minus_a[s][:],
+                in0=penalty[:, s // H : s // H + 1, :].to_broadcast([P, TILES, S]),
+                in1=minus_a[s][:],
+                op=ALU.subtract,
+            )
+
+        def row_maximum(s):
+            minus_max[s] = four.tile([P, TILES], F32, name="minus_max")
+            nc.vector.tensor_reduce(out=minus_max[s][:], in_=minus_a[s][:], axis=AXIS.X, op=ALU.min)
+
+        def exponentials(s):
+            e = pair.tile([P, TILES * S], BF16)
+            row_sum[s] = four.tile([P, TILES], F32, name="row_sum")
+            for n in range(TILES):
+                nc.scalar.activation(
+                    out=e[:, n * S : (n + 1) * S],
+                    in_=minus_a[s][:, n, :],
+                    func=ACT.Exp,
+                    scale=-1.0,
+                    bias=minus_max[s][:, n : n + 1],
+                    accum_out=row_sum[s][:, n : n + 1],
+                )
+            e_words = e[:].bitcast(F32)
+            for half in range(2):
+                e_turned[s, half] = word_banks.tile([P, 2, 2, P], F32, name="e_turned", tag="turned")
+                for u in range(2):
+                    for m in range(2):
+                        first = (2 * half + m) * (S // 2) + u * P
+                        nc.tensor.transpose(
+                            e_turned[s, half][:, u, m, :], e_words[:, first : first + P], ident_f32[:]
+                        )
+
+        def project_v(s):
+            b, h = divmod(s, H)
+            v_bank[s] = product_banks.tile([P, TILES, DH], F32, name="v_bank", tag="product")
+            for t in range(TILES):
+                for g in range(PASSES):
+                    nc.tensor.matmul_mx(
+                        out=v_bank[s][:, t, :],
+                        lhsT=x_codes[:, b * TILES + t, g, :].bitcast(FP8X4),
+                        lhsT_scale=x_scales[:, b * TILES + t, g, :],
+                        rhs=wv_codes[:, h, g, :].bitcast(FP8X4),
+                        rhs_scale=wv_scales[:, h, g, :],
+                        start=(g == 0),
+                        stop=(g == PASSES - 1),
+                    )
+
+        def round_v(s):
+            v_grouped[s] = pair.tile([P, DH * 4], BF16, name="v_grouped", align_bytes=64)
+            nc.scalar.copy(
+                out=v_grouped[s][:].rearrange("p (c t) -> p c t", t=TILES),
+                in_=v_bank[s][:].rearrange("p t c -> p c t"),
+            )
+
+        def quantise_v(s):
+            nc.vector.quantize_mx(
+                out=v_codes[:, s, :].bitcast(FP8X4), scales=v_scales[:, s, :], in_=v_grouped[s][:]
+            )
+
+        for step in range(HEADS + ATTEND):
+
+            def head(stage):
+                s = step - stage
+                return s if 0 <= s < HEADS else None
+
+            s = head(ATTEND)
+            if s is not None:
+                e_grouped = pair.tile([P, S * 4], BF16, align_bytes=64)
+                e_grouped_words = e_grouped[:].bitcast(F32).rearrange("p (i u) -> p i u", u=2)
+                for half in range(2):
+                    nc.vector.tensor_copy(
+                        out=e_grouped_words[:, 2 * P * half : 2 * P * (half + 1), :],
+                        in_=e_turned[s, half][:].rearrange("p u m i -> p (m i) u"),
+                    )
+            if head(TURN_QK) is not None:
+                turn_qk(head(TURN_QK))
+            if s is not None:
+                e_codes = pair.tile([P, S], U32, align_bytes=64)
+                e_scales = pair.tile([P, S], U8, align_bytes=64)
+                nc.vector.quantize_mx(out=e_codes[:].bitcast(FP8X4), scales=e_scales[:], in_=e_grouped[:])
+            if head(TANH) is not None:
+                tanh_and_mask(head(TANH))
+            if head(PROJECT_V + 1) is not None:
+                round_v(head(PROJECT_V + 1))
+            if s is not None:
+                o_bank = product_banks.tile([P, TILES, DH], F32, tag="product")
+                for n in range(TILES):
+                    nc.tensor.matmul_mx(
+                        out=o_bank[:, n, :],
+                        lhsT=e_codes[:, n * P : (n + 1) * P].bitcast(FP8X4),
+                        lhsT_scale=e_scales[:, n * P : (n + 1) * P],
+                        rhs=v_codes[:, s, :].bitcast(FP8X4),
+                        rhs_scale=v_scales[:, s, :],
+                        start=True,
+                        stop=True,
+                    )
+            if head(ROW_MAX) is not None:
+                row_maximum(head(ROW_MAX))
+            if head(MULTIPLY_QK) is not None:
+                multiply_qk(head(MULTIPLY_QK))
+            if s is not None:
+                inverse = pair.tile([P, TILES], F32)
+                nc.vector.reciprocal(out=inverse[:], in_=row_sum[s][:])
+                o = trio.tile([P, TILES, DH], F32)
+                nc.vector.tensor_tensor(
+                    out=o[:],
+                    in0=o_bank[:],
+                    in1=inverse[:].unsqueeze(2).to_broadcast([P, TILES, DH]),
+                    op=ALU.mult,
+                )
+                b, h = divmod(s, H)
+                nc.sync.dma_start(
+                    out=out[:, b, h * DH : (h + 1) * DH].rearrange("(p n) c -> p n c", n=TILES), in_=o[:]
+                )
+            if head(PROJECT_V + 1) is not None:
+                quantise_v(head(PROJECT_V + 1))
+            first_block = ROWS_PER_STEP * (step - FIRST_ROWS_STEP)
+            if 0 <= first_block < len(row_blocks):
+                for rows_words, codes, scales in row_blocks[first_block : first_block + ROWS_PER_STEP]:
+                    quantise_rows(rows_words, codes, scales)
+            if head(EXP) is not None:
+                exponentials(head(EXP))
+            if head(PROJECT_V) is not None:
+                project_v(head(PROJECT_V))

@@ -20,15 +20,14 @@ TILES = S // P
 PASSES = D // 512
 FLOPS = 2 * (S * B) * (H * DH) * D + 2 * 2 * HEADS * S * S * DH
 
-TURN_QK = 0
-MULTIPLY_QK = 1
-TANH = 2
-PROJECT_V = 3
+TURN_QK = 1
+TANH = 3
 ROW_MAX = 4
 EXP = 5
 ATTEND = 6
-FIRST_ROWS_STEP = 2
-ROWS_PER_STEP = 4
+STORE = 7
+SCORE_BANKS = 3
+ROWS_STEPS = (3, 4)
 
 
 def tile_attention_pa_kernel(tc, q, k, x, wv, mask, out):
@@ -38,10 +37,8 @@ def tile_attention_pa_kernel(tc, q, k, x, wv, mask, out):
         pair = stack.enter_context(tc.tile_pool(name="pair", bufs=2))
         trio = stack.enter_context(tc.tile_pool(name="trio", bufs=3))
         four = stack.enter_context(tc.tile_pool(name="four", bufs=4))
-        score_banks = stack.enter_context(tc.psum_pool(name="score_banks", bufs=4))
+        score_banks = stack.enter_context(tc.psum_pool(name="score_banks", bufs=SCORE_BANKS))
         qk_banks = stack.enter_context(tc.psum_pool(name="qk_banks", bufs=1))
-        word_banks = stack.enter_context(tc.psum_pool(name="word_banks", bufs=2))
-        product_banks = stack.enter_context(tc.psum_pool(name="product_banks", bufs=1))
         stack.enter_context(tc.manual_schedule())
 
         ident_bf16 = keep.tile([P, P], BF16)
@@ -87,131 +84,49 @@ def tile_attention_pa_kernel(tc, q, k, x, wv, mask, out):
 
         x_words = x_sb[:].bitcast(F32).rearrange("p u (e b w) -> p u e b w", e=2, b=B)
         wv_words = wv_sb[:].bitcast(F32)
-        x_codes = keep.tile([P, B * TILES, PASSES, P], U32, align_bytes=64)
-        x_scales = keep.tile([P, B * TILES, PASSES, P], U8, align_bytes=64)
-        wv_codes = keep.tile([P, H, PASSES, DH], U32, align_bytes=64)
-        wv_scales = keep.tile([P, H, PASSES, DH], U8, align_bytes=64)
+        x_codes = keep.tile([P, B, TILES, PASSES, P], U32, align_bytes=64)
+        x_scales = keep.tile([P, B, TILES, PASSES, P], U8, align_bytes=64)
+        wv_codes = keep.tile([P, 2, 4, PASSES, DH], U32, align_bytes=64)
+        wv_scales = keep.tile([P, 2, 4, PASSES, DH], U8, align_bytes=64)
         v_codes = keep.tile([P, HEADS, DH], U32, align_bytes=64)
         v_scales = keep.tile([P, HEADS, DH], U8, align_bytes=64)
 
-        row_blocks = []
-        for t in range(TILES):
-            row_blocks.append((x_words[:, t // 2, t % 2, 0, :], x_codes[:, t], x_scales[:, t]))
-        for h in range(H):
-            row_blocks.append((wv_words[:, h, :], wv_codes[:, h], wv_scales[:, h]))
-        for t in range(TILES):
-            row_blocks.append(
-                (x_words[:, t // 2, t % 2, 1, :], x_codes[:, TILES + t], x_scales[:, TILES + t])
-            )
+        def turn_four(row_banks, blocks):
+            grouped = pair.tile([P, 4 * PASSES * P * 4], BF16, align_bytes=64)
+            grouped_words = grouped[:].bitcast(F32).rearrange("p (r g c u) -> p r g c u", r=4, g=PASSES, u=2)
+            for r in range(4):
+                turned = row_banks.tile([P, 2, PASSES, P], F32)
+                for g in range(PASSES):
+                    for u in range(2):
+                        first = 256 * g + 128 * u
+                        nc.tensor.transpose(turned[:, u, g, :], blocks[r][:, first : first + P], ident_f32[:])
+                copy = nc.scalar.copy if r % 2 == 0 else nc.vector.tensor_copy
+                copy(out=grouped_words[:, r], in_=turned[:].rearrange("p u g c -> p g c u"))
+            return grouped
 
-        def quantise_rows(rows_words, codes, scales):
-            turned = word_banks.tile([P, 2, PASSES, P], F32, tag="turned")
-            for g in range(PASSES):
-                for u in range(2):
-                    first = 256 * g + 128 * u
-                    nc.tensor.transpose(turned[:, u, g, :], rows_words[:, first : first + P], ident_f32[:])
-            grouped = trio.tile([P, PASSES * P * 4], BF16, align_bytes=64)
-            nc.scalar.copy(
-                out=grouped[:].bitcast(F32).rearrange("p (g c u) -> p g c u", g=PASSES, u=2),
-                in_=turned[:].rearrange("p u g c -> p g c u"),
-            )
+        def quantise_four(grouped, codes, scales):
             nc.vector.quantize_mx(
-                out=codes.rearrange("p g c -> p (g c)").bitcast(FP8X4),
-                scales=scales.rearrange("p g c -> p (g c)"),
+                out=codes.rearrange("p r g c -> p (r g c)").bitcast(FP8X4),
+                scales=scales.rearrange("p r g c -> p (r g c)"),
                 in_=grouped[:],
             )
 
+        def quantise_x(row_banks):
+            grouped = [
+                turn_four(row_banks, [x_words[:, t // 2, t % 2, b, :] for t in range(TILES)]) for b in range(B)
+            ]
+            for b in range(B):
+                quantise_four(grouped[b], x_codes[:, b], x_scales[:, b])
+
+        def quantise_wv(row_banks):
+            grouped = [turn_four(row_banks, [wv_words[:, 4 * f + r, :] for r in range(4)]) for f in range(2)]
+            for f in range(2):
+                quantise_four(grouped[f], wv_codes[:, f], wv_scales[:, f])
+
         qk_turned, score, minus_a, minus_max, row_sum = {}, {}, {}, {}, {}
-        e_turned, v_bank, v_grouped = {}, {}, {}
+        e_turned, e_codes, e_scales, v_grouped, o_bank = {}, {}, {}, {}, {}
 
-        def turn_qk(s):
-            bank = qk_banks.tile([P, 2 * TILES, P], BF16)
-            for n in range(TILES):
-                nc.tensor.transpose(bank[:, n, :], q_sb[:, s, n, :], ident_bf16[:])
-            for n in range(TILES):
-                nc.tensor.transpose(bank[:, TILES + n, :], k_sb[:, s, n, :], ident_bf16[:])
-            qk_turned[s] = pair.tile([P, 2 * TILES, P], BF16, name="qk_turned")
-            nc.vector.tensor_copy(out=qk_turned[s][:], in_=bank[:])
-
-        def multiply_qk(s):
-            for n in range(TILES):
-                score[s, n] = score_banks.tile([P, S], F32, name="score")
-                nc.tensor.matmul(
-                    out=score[s, n][:],
-                    lhsT=qk_turned[s][:, n, :],
-                    rhs=qk_turned[s][:, TILES : 2 * TILES, :].rearrange("p n t -> p (n t)"),
-                    start=True,
-                    stop=True,
-                )
-
-        def tanh_and_mask(s):
-            minus_a[s] = four.tile([P, TILES, S], F32, name="minus_a")
-            for n in range(TILES):
-                nc.scalar.activation(
-                    out=minus_a[s][:, n, :], in_=score[s, n][:], func=ACT.Tanh, scale=1.0 / math.sqrt(DH)
-                )
-            nc.gpsimd.tensor_tensor(
-                out=minus_a[s][:],
-                in0=penalty[:, s // H : s // H + 1, :].to_broadcast([P, TILES, S]),
-                in1=minus_a[s][:],
-                op=ALU.subtract,
-            )
-
-        def row_maximum(s):
-            minus_max[s] = four.tile([P, TILES], F32, name="minus_max")
-            nc.vector.tensor_reduce(out=minus_max[s][:], in_=minus_a[s][:], axis=AXIS.X, op=ALU.min)
-
-        def exponentials(s):
-            e = pair.tile([P, TILES * S], BF16)
-            row_sum[s] = four.tile([P, TILES], F32, name="row_sum")
-            for n in range(TILES):
-                nc.scalar.activation(
-                    out=e[:, n * S : (n + 1) * S],
-                    in_=minus_a[s][:, n, :],
-                    func=ACT.Exp,
-                    scale=-1.0,
-                    bias=minus_max[s][:, n : n + 1],
-                    accum_out=row_sum[s][:, n : n + 1],
-                )
-            e_words = e[:].bitcast(F32)
-            for half in range(2):
-                e_turned[s, half] = word_banks.tile([P, 2, 2, P], F32, name="e_turned", tag="turned")
-                for u in range(2):
-                    for m in range(2):
-                        first = (2 * half + m) * (S // 2) + u * P
-                        nc.tensor.transpose(
-                            e_turned[s, half][:, u, m, :], e_words[:, first : first + P], ident_f32[:]
-                        )
-
-        def project_v(s):
-            b, h = divmod(s, H)
-            v_bank[s] = product_banks.tile([P, TILES, DH], F32, name="v_bank", tag="product")
-            for t in range(TILES):
-                for g in range(PASSES):
-                    nc.tensor.matmul_mx(
-                        out=v_bank[s][:, t, :],
-                        lhsT=x_codes[:, b * TILES + t, g, :].bitcast(FP8X4),
-                        lhsT_scale=x_scales[:, b * TILES + t, g, :],
-                        rhs=wv_codes[:, h, g, :].bitcast(FP8X4),
-                        rhs_scale=wv_scales[:, h, g, :],
-                        start=(g == 0),
-                        stop=(g == PASSES - 1),
-                    )
-
-        def round_v(s):
-            v_grouped[s] = pair.tile([P, DH * 4], BF16, name="v_grouped", align_bytes=64)
-            nc.scalar.copy(
-                out=v_grouped[s][:].rearrange("p (c t) -> p c t", t=TILES),
-                in_=v_bank[s][:].rearrange("p t c -> p c t"),
-            )
-
-        def quantise_v(s):
-            nc.vector.quantize_mx(
-                out=v_codes[:, s, :].bitcast(FP8X4), scales=v_scales[:, s, :], in_=v_grouped[s][:]
-            )
-
-        for step in range(HEADS + ATTEND):
-
+        def one_step(step, row_banks, e_banks, v_banks, o_banks):
             def head(stage):
                 s = step - stage
                 return s if 0 <= s < HEADS else None
@@ -225,39 +140,15 @@ def tile_attention_pa_kernel(tc, q, k, x, wv, mask, out):
                         out=e_grouped_words[:, 2 * P * half : 2 * P * (half + 1), :],
                         in_=e_turned[s, half][:].rearrange("p u m i -> p (m i) u"),
                     )
-            if head(TURN_QK) is not None:
-                turn_qk(head(TURN_QK))
-            if s is not None:
-                e_codes = pair.tile([P, S], U32, align_bytes=64)
-                e_scales = pair.tile([P, S], U8, align_bytes=64)
-                nc.vector.quantize_mx(out=e_codes[:].bitcast(FP8X4), scales=e_scales[:], in_=e_grouped[:])
-            if head(TANH) is not None:
-                tanh_and_mask(head(TANH))
-            if head(PROJECT_V + 1) is not None:
-                round_v(head(PROJECT_V + 1))
-            if s is not None:
-                o_bank = product_banks.tile([P, TILES, DH], F32, tag="product")
-                for n in range(TILES):
-                    nc.tensor.matmul_mx(
-                        out=o_bank[:, n, :],
-                        lhsT=e_codes[:, n * P : (n + 1) * P].bitcast(FP8X4),
-                        lhsT_scale=e_scales[:, n * P : (n + 1) * P],
-                        rhs=v_codes[:, s, :].bitcast(FP8X4),
-                        rhs_scale=v_scales[:, s, :],
-                        start=True,
-                        stop=True,
-                    )
-            if head(ROW_MAX) is not None:
-                row_maximum(head(ROW_MAX))
-            if head(MULTIPLY_QK) is not None:
-                multiply_qk(head(MULTIPLY_QK))
+
+            s = head(STORE)
             if s is not None:
                 inverse = pair.tile([P, TILES], F32)
                 nc.vector.reciprocal(out=inverse[:], in_=row_sum[s][:])
                 o = trio.tile([P, TILES, DH], F32)
                 nc.vector.tensor_tensor(
                     out=o[:],
-                    in0=o_bank[:],
+                    in0=o_bank[s][:],
                     in1=inverse[:].unsqueeze(2).to_broadcast([P, TILES, DH]),
                     op=ALU.mult,
                 )
@@ -265,13 +156,131 @@ def tile_attention_pa_kernel(tc, q, k, x, wv, mask, out):
                 nc.sync.dma_start(
                     out=out[:, b, h * DH : (h + 1) * DH].rearrange("(p n) c -> p n c", n=TILES), in_=o[:]
                 )
-            if head(PROJECT_V + 1) is not None:
-                quantise_v(head(PROJECT_V + 1))
-            first_block = ROWS_PER_STEP * (step - FIRST_ROWS_STEP)
-            if 0 <= first_block < len(row_blocks):
-                for rows_words, codes, scales in row_blocks[first_block : first_block + ROWS_PER_STEP]:
-                    quantise_rows(rows_words, codes, scales)
-            if head(EXP) is not None:
-                exponentials(head(EXP))
-            if head(PROJECT_V) is not None:
-                project_v(head(PROJECT_V))
+
+            s = head(TURN_QK)
+            if s is not None:
+                bank = qk_banks.tile([P, 2 * TILES, P], BF16)
+                for n in range(TILES):
+                    nc.tensor.transpose(bank[:, n, :], q_sb[:, s, n, :], ident_bf16[:])
+                for n in range(TILES):
+                    nc.tensor.transpose(bank[:, TILES + n, :], k_sb[:, s, n, :], ident_bf16[:])
+                qk_turned[s] = trio.tile([P, 2 * TILES, P], BF16, name="qk_turned")
+                nc.vector.tensor_copy(out=qk_turned[s][:], in_=bank[:])
+
+            s = head(ATTEND)
+            if s is not None:
+                e_codes[s] = pair.tile([P, S], U32, name="e_codes", align_bytes=64)
+                e_scales[s] = pair.tile([P, S], U8, name="e_scales", align_bytes=64)
+                nc.vector.quantize_mx(out=e_codes[s][:].bitcast(FP8X4), scales=e_scales[s][:], in_=e_grouped[:])
+                nc.vector.quantize_mx(
+                    out=v_codes[:, s, :].bitcast(FP8X4), scales=v_scales[:, s, :], in_=v_grouped[s][:]
+                )
+
+            for n in range(TILES):
+                tile_now = TILES * (step - TANH) + n
+                if 0 <= tile_now < HEADS * TILES:
+                    s = tile_now // TILES
+                    if n == 0:
+                        minus_a[s] = trio.tile([P, TILES, S], F32, name="minus_a")
+                    nc.scalar.activation(
+                        out=minus_a[s][:, n, :], in_=score[tile_now][:], func=ACT.Tanh, scale=1.0 / math.sqrt(DH)
+                    )
+                tile_next = tile_now + SCORE_BANKS
+                if 0 <= tile_next < HEADS * TILES:
+                    s, m = divmod(tile_next, TILES)
+                    score[tile_next] = score_banks.tile([P, S], F32, name="score")
+                    nc.tensor.matmul(
+                        out=score[tile_next][:],
+                        lhsT=qk_turned[s][:, m, :],
+                        rhs=qk_turned[s][:, TILES : 2 * TILES, :].rearrange("p n t -> p (n t)"),
+                        start=True,
+                        stop=True,
+                    )
+
+            s = head(TANH)
+            if s is not None:
+                nc.gpsimd.tensor_tensor(
+                    out=minus_a[s][:],
+                    in0=penalty[:, s // H : s // H + 1, :].to_broadcast([P, TILES, S]),
+                    in1=minus_a[s][:],
+                    op=ALU.subtract,
+                )
+
+            s = head(ROW_MAX)
+            if s is not None:
+                minus_max[s] = trio.tile([P, TILES], F32, name="minus_max")
+                nc.vector.tensor_reduce(out=minus_max[s][:], in_=minus_a[s][:], axis=AXIS.X, op=ALU.min)
+
+            if step == ROWS_STEPS[0]:
+                quantise_x(row_banks)
+            if step == ROWS_STEPS[1]:
+                quantise_wv(row_banks)
+
+            s = head(EXP)
+            if s is not None:
+                b, h = divmod(s, H)
+                v_bank = v_banks.tile([P, TILES, DH], F32)
+                for t in range(TILES):
+                    for g in range(PASSES):
+                        nc.tensor.matmul_mx(
+                            out=v_bank[:, t, :],
+                            lhsT=x_codes[:, b, t, g, :].bitcast(FP8X4),
+                            lhsT_scale=x_scales[:, b, t, g, :],
+                            rhs=wv_codes[:, h // 4, h % 4, g, :].bitcast(FP8X4),
+                            rhs_scale=wv_scales[:, h // 4, h % 4, g, :],
+                            start=(g == 0),
+                            stop=(g == PASSES - 1),
+                        )
+                e = pair.tile([P, TILES * S], BF16)
+                row_sum[s] = four.tile([P, TILES], F32, name="row_sum")
+                for n in range(TILES):
+                    nc.scalar.activation(
+                        out=e[:, n * S : (n + 1) * S],
+                        in_=minus_a[s][:, n, :],
+                        func=ACT.Exp,
+                        scale=-1.0,
+                        bias=minus_max[s][:, n : n + 1],
+                        accum_out=row_sum[s][:, n : n + 1],
+                    )
+                e_words = e[:].bitcast(F32)
+
+            for half in range(2):
+                s = head(EXP)
+                if s is not None:
+                    e_turned[s, half] = e_banks.tile([P, 2, 2, P], F32, name="e_turned")
+                    for u in range(2):
+                        for m in range(2):
+                            first = (2 * half + m) * (S // 2) + u * P
+                            nc.tensor.transpose(
+                                e_turned[s, half][:, u, m, :], e_words[:, first : first + P], ident_f32[:]
+                            )
+                s = head(ATTEND) if half == 0 else None
+                if s is not None:
+                    o_bank[s] = o_banks.tile([P, TILES, DH], F32, name="o_bank")
+                    for n in range(TILES):
+                        nc.tensor.matmul_mx(
+                            out=o_bank[s][:, n, :],
+                            lhsT=e_codes[s][:, n * P : (n + 1) * P].bitcast(FP8X4),
+                            lhsT_scale=e_scales[s][:, n * P : (n + 1) * P],
+                            rhs=v_codes[:, s, :].bitcast(FP8X4),
+                            rhs_scale=v_scales[:, s, :],
+                            start=True,
+                            stop=True,
+                        )
+                s = head(EXP) if half == 0 else None
+                if s is not None:
+                    v_grouped[s] = pair.tile([P, DH * 4], BF16, name="v_grouped", align_bytes=64)
+                    nc.scalar.copy(
+                        out=v_grouped[s][:].rearrange("p (c t) -> p c t", t=TILES),
+                        in_=v_bank[:].rearrange("p t c -> p c t"),
+                    )
+
+        with tc.psum_pool(name="row_banks", bufs=4) as row_banks:
+            for step in range(EXP):
+                one_step(step, row_banks, None, None, None)
+        with ExitStack() as late:
+            e_banks = late.enter_context(tc.psum_pool(name="e_banks", bufs=2, reuse_waits="tile"))
+            v_banks = late.enter_context(tc.psum_pool(name="v_banks", bufs=1, reuse_waits="tile"))
+            o_banks = late.enter_context(tc.psum_pool(name="o_banks", bufs=1, reuse_waits="tile"))
+            for step in range(EXP, HEADS + STORE):
+                one_step(step, None, e_banks, v_banks, o_banks)

@@ -199,7 +199,7 @@ def tile_attention_pa_kernel(tc, q, k, x, wv, mask, out):
 
             s = head(TANH)
             if s is not None:
-                nc.gpsimd.tensor_tensor(
+                nc.vector.tensor_tensor(
                     out=minus_a[s][:],
                     in0=penalty[:, s // H : s // H + 1, :].to_broadcast([P, TILES, S]),
                     in1=minus_a[s][:],

@@ -24,8 +24,8 @@ TURN_QK = 1
 TANH = 3
 ROW_MAX = 4
 EXP = 5
-ATTEND = 6
-STORE = 7
+QUANTISE = 6
+ATTEND = 7
 SCORE_BANKS = 3
 ROWS_STEPS = (3, 4)
 
@@ -124,7 +124,7 @@ def tile_attention_pa_kernel(tc, q, k, x, wv, mask, out):
                 quantise_four(grouped[f], wv_codes[:, f], wv_scales[:, f])
 
         qk_turned, score, minus_a, minus_max, row_sum = {}, {}, {}, {}, {}
-        e_turned, e_codes, e_scales, v_grouped, o_bank = {}, {}, {}, {}, {}
+        e_turned, e_codes, e_scales, v_grouped = {}, {}, {}, {}
 
         def one_step(step, row_banks, e_banks, v_banks, o_banks):
             def head(stage):
@@ -133,47 +133,41 @@ def tile_attention_pa_kernel(tc, q, k, x, wv, mask, out):
 
             s = head(ATTEND)
             if s is not None:
-                e_grouped = pair.tile([P, S * 4], BF16, align_bytes=64)
-                e_grouped_words = e_grouped[:].bitcast(F32).rearrange("p (i u) -> p i u", u=2)
-                for half in range(2):
-                    nc.vector.tensor_copy(
-                        out=e_grouped_words[:, 2 * P * half : 2 * P * (half + 1), :],
-                        in_=e_turned[s, half][:].rearrange("p u m i -> p (m i) u"),
+                o_bank = o_banks.tile([P, TILES, DH], F32)
+                for n in range(TILES):
+                    nc.tensor.matmul_mx(
+                        out=o_bank[:, n, :],
+                        lhsT=e_codes[s][:, n * P : (n + 1) * P].bitcast(FP8X4),
+                        lhsT_scale=e_scales[s][:, n * P : (n + 1) * P],
+                        rhs=v_codes[:, s, :].bitcast(FP8X4),
+                        rhs_scale=v_scales[:, s, :],
+                        start=True,
+                        stop=True,
                     )
 
-            s = head(STORE)
+            s = head(ROW_MAX)
+            if s is not None:
+                nc.vector.tensor_tensor(
+                    out=minus_a[s][:],
+                    in0=penalty[:, s // H : s // H + 1, :].to_broadcast([P, TILES, S]),
+                    in1=minus_a[s][:],
+                    op=ALU.subtract,
+                )
+
+            s = head(ATTEND)
             if s is not None:
                 inverse = pair.tile([P, TILES], F32)
                 nc.vector.reciprocal(out=inverse[:], in_=row_sum[s][:])
                 o = trio.tile([P, TILES, DH], F32)
                 nc.vector.tensor_tensor(
                     out=o[:],
-                    in0=o_bank[s][:],
+                    in0=o_bank[:],
                     in1=inverse[:].unsqueeze(2).to_broadcast([P, TILES, DH]),
                     op=ALU.mult,
                 )
                 b, h = divmod(s, H)
                 nc.sync.dma_start(
                     out=out[:, b, h * DH : (h + 1) * DH].rearrange("(p n) c -> p n c", n=TILES), in_=o[:]
-                )
-
-            s = head(TURN_QK)
-            if s is not None:
-                bank = qk_banks.tile([P, 2 * TILES, P], BF16)
-                for n in range(TILES):
-                    nc.tensor.transpose(bank[:, n, :], q_sb[:, s, n, :], ident_bf16[:])
-                for n in range(TILES):
-                    nc.tensor.transpose(bank[:, TILES + n, :], k_sb[:, s, n, :], ident_bf16[:])
-                qk_turned[s] = trio.tile([P, 2 * TILES, P], BF16, name="qk_turned")
-                nc.vector.tensor_copy(out=qk_turned[s][:], in_=bank[:])
-
-            s = head(ATTEND)
-            if s is not None:
-                e_codes[s] = pair.tile([P, S], U32, name="e_codes", align_bytes=64)
-                e_scales[s] = pair.tile([P, S], U8, name="e_scales", align_bytes=64)
-                nc.vector.quantize_mx(out=e_codes[s][:].bitcast(FP8X4), scales=e_scales[s][:], in_=e_grouped[:])
-                nc.vector.quantize_mx(
-                    out=v_codes[:, s, :].bitcast(FP8X4), scales=v_scales[:, s, :], in_=v_grouped[s][:]
                 )
 
             for n in range(TILES):
@@ -197,19 +191,36 @@ def tile_attention_pa_kernel(tc, q, k, x, wv, mask, out):
                         stop=True,
                     )
 
-            s = head(TANH)
-            if s is not None:
-                nc.vector.tensor_tensor(
-                    out=minus_a[s][:],
-                    in0=penalty[:, s // H : s // H + 1, :].to_broadcast([P, TILES, S]),
-                    in1=minus_a[s][:],
-                    op=ALU.subtract,
-                )
-
             s = head(ROW_MAX)
             if s is not None:
                 minus_max[s] = trio.tile([P, TILES], F32, name="minus_max")
                 nc.vector.tensor_reduce(out=minus_max[s][:], in_=minus_a[s][:], axis=AXIS.X, op=ALU.min)
+
+            s = head(TURN_QK)
+            if s is not None:
+                bank = qk_banks.tile([P, 2 * TILES, P], BF16)
+                for n in range(TILES):
+                    nc.tensor.transpose(bank[:, n, :], q_sb[:, s, n, :], ident_bf16[:])
+                for n in range(TILES):
+                    nc.tensor.transpose(bank[:, TILES + n, :], k_sb[:, s, n, :], ident_bf16[:])
+                qk_turned[s] = trio.tile([P, 2 * TILES, P], BF16, name="qk_turned")
+                nc.vector.tensor_copy(out=qk_turned[s][:], in_=bank[:])
+
+            s = head(QUANTISE)
+            if s is not None:
+                e_grouped = pair.tile([P, S * 4], BF16, align_bytes=64)
+                e_grouped_words = e_grouped[:].bitcast(F32).rearrange("p (i u) -> p i u", u=2)
+                for half in range(2):
+                    nc.scalar.copy(
+                        out=e_grouped_words[:, 2 * P * half : 2 * P * (half + 1), :],
+                        in_=e_turned[s, half][:].rearrange("p u m i -> p (m i) u"),
+                    )
+                e_codes[s] = pair.tile([P, S], U32, name="e_codes", align_bytes=64)
+                e_scales[s] = pair.tile([P, S], U8, name="e_scales", align_bytes=64)
+                nc.vector.quantize_mx(out=e_codes[s][:].bitcast(FP8X4), scales=e_scales[s][:], in_=e_grouped[:])
+                nc.vector.quantize_mx(
+                    out=v_codes[:, s, :].bitcast(FP8X4), scales=v_scales[:, s, :], in_=v_grouped[s][:]
+                )
 
             if step == ROWS_STEPS[0]:
                 quantise_x(row_banks)
@@ -242,11 +253,13 @@ def tile_attention_pa_kernel(tc, q, k, x, wv, mask, out):
                         bias=minus_max[s][:, n : n + 1],
                         accum_out=row_sum[s][:, n : n + 1],
                     )
+                v_grouped[s] = pair.tile([P, DH * 4], BF16, name="v_grouped", align_bytes=64)
+                nc.scalar.copy(
+                    out=v_grouped[s][:].rearrange("p (c t) -> p c t", t=TILES),
+                    in_=v_bank[:].rearrange("p t c -> p c t"),
+                )
                 e_words = e[:].bitcast(F32)
-
-            for half in range(2):
-                s = head(EXP)
-                if s is not None:
+                for half in range(2):
                     e_turned[s, half] = e_banks.tile([P, 2, 2, P], F32, name="e_turned")
                     for u in range(2):
                         for m in range(2):
@@ -254,26 +267,6 @@ def tile_attention_pa_kernel(tc, q, k, x, wv, mask, out):
                             nc.tensor.transpose(
                                 e_turned[s, half][:, u, m, :], e_words[:, first : first + P], ident_f32[:]
                             )
-                s = head(ATTEND) if half == 0 else None
-                if s is not None:
-                    o_bank[s] = o_banks.tile([P, TILES, DH], F32, name="o_bank")
-                    for n in range(TILES):
-                        nc.tensor.matmul_mx(
-                            out=o_bank[s][:, n, :],
-                            lhsT=e_codes[s][:, n * P : (n + 1) * P].bitcast(FP8X4),
-                            lhsT_scale=e_scales[s][:, n * P : (n + 1) * P],
-                            rhs=v_codes[:, s, :].bitcast(FP8X4),
-                            rhs_scale=v_scales[:, s, :],
-                            start=True,
-                            stop=True,
-                        )
-                s = head(EXP) if half == 0 else None
-                if s is not None:
-                    v_grouped[s] = pair.tile([P, DH * 4], BF16, name="v_grouped", align_bytes=64)
-                    nc.scalar.copy(
-                        out=v_grouped[s][:].rearrange("p (c t) -> p c t", t=TILES),
-                        in_=v_bank[:].rearrange("p t c -> p c t"),
-                    )
 
         with tc.psum_pool(name="row_banks", bufs=4) as row_banks:
             for step in range(EXP):
@@ -282,5 +275,5 @@ def tile_attention_pa_kernel(tc, q, k, x, wv, mask, out):
             e_banks = late.enter_context(tc.psum_pool(name="e_banks", bufs=2, reuse_waits="tile"))
             v_banks = late.enter_context(tc.psum_pool(name="v_banks", bufs=1, reuse_waits="tile"))
             o_banks = late.enter_context(tc.psum_pool(name="o_banks", bufs=1, reuse_waits="tile"))
-            for step in range(EXP, HEADS + STORE):
+            for step in range(EXP, HEADS + ATTEND + 1):
                 one_step(step, None, e_banks, v_banks, o_banks)

@@ -17,17 +17,19 @@ P = 128
 S, B, D, H, DH = 512, 2, 1024, 8, 128
 HEADS = B * H
 TILES = S // P
+ALL_TILES = HEADS * TILES
 PASSES = D // 512
 FLOPS = 2 * (S * B) * (H * DH) * D + 2 * 2 * HEADS * S * S * DH
 
-TURN_QK = 1
-TANH = 3
-ROW_MAX = 4
-EXP = 5
-QUANTISE = 6
-ATTEND = 7
-SCORE_BANKS = 3
-ROWS_STEPS = (3, 4)
+SCORE_AHEAD = 3
+MAX_BEHIND = 1
+EXP_BEHIND = 3
+TURN_AHEAD = 6
+ROWS_FROM = 3
+HEAD_STEP = 3
+LAST_HEAD = ALL_TILES + 2
+HEADS_FROM = LAST_HEAD - HEAD_STEP * (HEADS - 1)
+SLOTS = LAST_HEAD + 6
 
 
 def tile_attention_pa_kernel(tc, q, k, x, wv, mask, out):
@@ -36,244 +38,353 @@ def tile_attention_pa_kernel(tc, q, k, x, wv, mask, out):
         keep = stack.enter_context(tc.tile_pool(name="keep", bufs=1))
         pair = stack.enter_context(tc.tile_pool(name="pair", bufs=2))
         trio = stack.enter_context(tc.tile_pool(name="trio", bufs=3))
-        four = stack.enter_context(tc.tile_pool(name="four", bufs=4))
-        score_banks = stack.enter_context(tc.psum_pool(name="score_banks", bufs=SCORE_BANKS))
+        five = stack.enter_context(tc.tile_pool(name="five", bufs=5))
+        eight = stack.enter_context(tc.tile_pool(name="eight", bufs=8))
+        score_banks = stack.enter_context(tc.psum_pool(name="score_banks", bufs=SCORE_AHEAD))
         qk_banks = stack.enter_context(tc.psum_pool(name="qk_banks", bufs=1))
+        e_banks = stack.enter_context(tc.psum_pool(name="e_banks", bufs=2))
+        mixed_banks = stack.enter_context(tc.psum_pool(name="mixed_banks", bufs=2))
         stack.enter_context(tc.manual_schedule())
 
+        q_sb = keep.tile([P, HEADS, TILES, DH], BF16)
+        k_sb = keep.tile([P, HEADS, 2, 2, DH], BF16)
+        q_rows = q.rearrange("b h (p n) d -> p (b h) n d", n=TILES)
+        k_rows = k.rearrange("b h (f p u) d -> p (b h) f u d", f=2, u=2)
+        x_sb = keep.tile([P, B, 4, D], BF16)
+        x_rows = x.rearrange("(p r) b d -> p b r d", r=4)
+        wv_sb = keep.tile([P, H, D], BF16)
+        wv_rows = wv.rearrange("h c d -> c h d")
+        mask_sb = keep.tile([P, B * S], BF16)
+        mask_rows = keep.tile([P, B, 4], BF16)
+
+        def load_qk(first, count):
+            heads = slice(first, first + count)
+            nc.sync.dma_start(out=k_sb[:, heads], in_=k_rows[:, heads])
+            nc.sync.dma_start(out=q_sb[:, heads], in_=q_rows[:, heads])
+
+        nc.vector.memset(mask_sb[:], 0.0)
+        nc.scalar.dma_start(out=mask_sb[0:1, :], in_=mask.rearrange("b t -> (b t)").unsqueeze(0))
+        load_qk(0, 1)
+        load_qk(1, 1)
+        load_qk(2, 1)
+        nc.sync.dma_start(out=x_sb[:, 0, 0:2], in_=x_rows[:, 0, 0:2])
+        nc.sync.dma_start(out=x_sb[:, 0, 2:4], in_=x_rows[:, 0, 2:4])
+        load_qk(3, 1)
+        nc.sync.dma_start(out=wv_sb[:, 0:4], in_=wv_rows[:, 0:4])
+        nc.sync.dma_start(out=mask_rows[:], in_=mask.rearrange("b (p r) -> p b r", r=4))
+        load_qk(4, 2)
+        nc.sync.dma_start(out=wv_sb[:, 4:8], in_=wv_rows[:, 4:8])
+        load_qk(6, 2)
+        nc.sync.dma_start(out=x_sb[:, 1], in_=x_rows[:, 1])
+        for first in range(8, HEADS, 2):
+            load_qk(first, 2)
+
+        ones = keep.tile([P, P], BF16)
+        nc.vector.memset(ones[:], 1.0)
         ident_bf16 = keep.tile([P, P], BF16)
         make_identity(nc, ident_bf16[:])
         ident_f32 = keep.tile([P, P], F32)
         make_identity(nc, ident_f32[:])
 
-        q_sb = keep.tile([P, HEADS, TILES, DH], BF16)
-        k_sb = keep.tile([P, HEADS, TILES, DH], BF16)
-        q_rows = q.rearrange("b h (p n) d -> p (b h) n d", n=TILES)
-        k_rows = k.rearrange("b h (n p) d -> p (b h) n d", p=P)
-        x_sb = keep.tile([P, 2, 2 * B * D], BF16)
-        x_rows = x.rearrange("(u p e) b d -> p u (e b d)", u=2, e=2)
-        wv_sb = keep.tile([P, H, D], BF16)
-        wv_rows = wv.rearrange("h c d -> c h d")
-        mask_sb = keep.tile([P, B * S], BF16)
+        kept = keep.tile([P, B, S], BF16)
+        kept_rows = keep.tile([P, B, 4], F32)
+        any_left = keep.tile([P, B], F32)
+        none_left = keep.tile([P, B], F32)
+        minus_masked = keep.tile([P, B], F32)
 
-        def load_qk(two):
-            heads = slice(2 * two, 2 * two + 2)
-            nc.sync.dma_start(out=q_sb[:, heads], in_=q_rows[:, heads])
-            nc.sync.dma_start(out=k_sb[:, heads], in_=k_rows[:, heads])
+        mask_bank = {}
 
-        load_qk(0)
-        nc.sync.dma_start(out=mask_sb[:], in_=mask.rearrange("b t -> (b t)").partition_broadcast(P))
-        load_qk(1)
-        nc.sync.dma_start(out=x_sb[:, 0], in_=x_rows[:, 0])
-        nc.sync.dma_start(out=x_sb[:, 1], in_=x_rows[:, 1])
-        nc.sync.dma_start(out=wv_sb[:, 0:4], in_=wv_rows[:, 0:4])
-        load_qk(2)
-        nc.sync.dma_start(out=wv_sb[:, 4:8], in_=wv_rows[:, 4:8])
-        for two in range(3, HEADS // 2):
-            load_qk(two)
+        def spread_mask(b):
+            mask_bank[b] = mixed_banks.tile([P, S], F32, name="mixed")
+            nc.tensor.matmul(
+                out=mask_bank[b][:], lhsT=ones[:], rhs=mask_sb[:, b * S : (b + 1) * S], start=True, stop=True
+            )
 
-        penalty = keep.tile([P, B, S], F32)
-        nc.vector.tensor_scalar(
-            out=penalty[:].rearrange("p b t -> p (b t)"),
-            in0=mask_sb[:],
-            scalar1=-10000.0,
-            scalar2=10000.0,
-            op0=ALU.mult,
-            op1=ALU.add,
-        )
+        def take_mask(b):
+            bank = mask_bank[b]
+            nc.vector.tensor_reduce(out=any_left[:, b : b + 1], in_=bank[:], axis=AXIS.X, op=ALU.max)
+            nc.vector.tensor_scalar(
+                out=none_left[:, b : b + 1],
+                in0=any_left[:, b : b + 1],
+                scalar1=-1.0,
+                scalar2=1.0,
+                op0=ALU.mult,
+                op1=ALU.add,
+            )
+            nc.vector.tensor_scalar(
+                out=kept[:, b, :].rearrange("p (u z) -> p u z", u=2),
+                in0=bank[:].rearrange("p (z u) -> p u z", u=2),
+                scalar1=none_left[:, b : b + 1],
+                scalar2=-float(S),
+                op0=ALU.max,
+                op1=ALU.add,
+                accum_out=minus_masked[:, b : b + 1],
+            )
 
-        x_words = x_sb[:].bitcast(F32).rearrange("p u (e b w) -> p u e b w", e=2, b=B)
+        def take_mask_rows(b):
+            nc.vector.tensor_scalar(
+                out=kept_rows[:, b, :].rearrange("p (u e) -> p u e", u=2),
+                in0=mask_rows[:, b, :].rearrange("p (e u) -> p u e", u=2),
+                scalar1=none_left[:, b : b + 1],
+                scalar2=None,
+                op0=ALU.max,
+            )
+
+        x_words = x_sb[:].bitcast(F32)
         wv_words = wv_sb[:].bitcast(F32)
-        x_codes = keep.tile([P, B, TILES, PASSES, P], U32, align_bytes=64)
-        x_scales = keep.tile([P, B, TILES, PASSES, P], U8, align_bytes=64)
+        x_codes = keep.tile([P, B, 4, PASSES, P], U32, align_bytes=64)
+        x_scales = keep.tile([P, B, 4, PASSES, P], U8, align_bytes=64)
         wv_codes = keep.tile([P, 2, 4, PASSES, DH], U32, align_bytes=64)
         wv_scales = keep.tile([P, 2, 4, PASSES, DH], U8, align_bytes=64)
         v_codes = keep.tile([P, HEADS, DH], U32, align_bytes=64)
         v_scales = keep.tile([P, HEADS, DH], U8, align_bytes=64)
 
-        def turn_four(row_banks, blocks):
-            grouped = pair.tile([P, 4 * PASSES * P * 4], BF16, align_bytes=64)
-            grouped_words = grouped[:].bitcast(F32).rearrange("p (r g c u) -> p r g c u", r=4, g=PASSES, u=2)
-            for r in range(4):
-                turned = row_banks.tile([P, 2, PASSES, P], F32)
-                for g in range(PASSES):
-                    for u in range(2):
-                        first = 256 * g + 128 * u
-                        nc.tensor.transpose(turned[:, u, g, :], blocks[r][:, first : first + P], ident_f32[:])
-                copy = nc.scalar.copy if r % 2 == 0 else nc.vector.tensor_copy
-                copy(out=grouped_words[:, r], in_=turned[:].rearrange("p u g c -> p g c u"))
-            return grouped
+        groups = [
+            ([x_words[:, 0, r, :] for r in range(4)], x_codes[:, 0], x_scales[:, 0]),
+            ([wv_words[:, r, :] for r in range(4)], wv_codes[:, 0], wv_scales[:, 0]),
+            ([wv_words[:, 4 + r, :] for r in range(4)], wv_codes[:, 1], wv_scales[:, 1]),
+            ([x_words[:, 1, r, :] for r in range(4)], x_codes[:, 1], x_scales[:, 1]),
+        ]
+        turned_rows, grouped_rows = {}, {}
 
-        def quantise_four(grouped, codes, scales):
+        def turn_rows(r):
+            block = groups[r // 4][0][r % 4]
+            turned_rows[r] = mixed_banks.tile([P, 2, PASSES, P], F32, name="mixed")
+            for g in range(PASSES):
+                for u in range(2):
+                    first = 256 * g + 128 * u
+                    nc.tensor.transpose(turned_rows[r][:, u, g, :], block[:, first : first + P], ident_f32[:])
+
+        def copy_rows(r):
+            if r % 4 == 0:
+                grouped_rows[r // 4] = pair.tile([P, 4 * PASSES * P * 4], BF16, name="grouped", align_bytes=64)
+            words = grouped_rows[r // 4][:].bitcast(F32).rearrange("p (r g c u) -> p r g c u", r=4, g=PASSES, u=2)
+            copy = nc.scalar.copy if r % 2 == 0 else nc.vector.tensor_copy
+            copy(out=words[:, r % 4], in_=turned_rows[r][:].rearrange("p u g c -> p g c u"))
+
+        def quantise_rows(group):
+            codes, scales = groups[group][1:]
             nc.vector.quantize_mx(
                 out=codes.rearrange("p r g c -> p (r g c)").bitcast(FP8X4),
                 scales=scales.rearrange("p r g c -> p (r g c)"),
-                in_=grouped[:],
+                in_=grouped_rows[group][:],
             )
 
-        def quantise_x(row_banks):
-            grouped = [
-                turn_four(row_banks, [x_words[:, t // 2, t % 2, b, :] for t in range(TILES)]) for b in range(B)
-            ]
-            for b in range(B):
-                quantise_four(grouped[b], x_codes[:, b], x_scales[:, b])
+        qk_turned, score, minus_a, minus_max, row_sum, masked_e = {}, {}, {}, {}, {}, {}
+        e, e_turned, e_grouped, e_codes, e_scales = {}, {}, {}, {}, {}
+        qk_bank, v_bank, v_grouped, o_bank = {}, {}, {}, {}
 
-        def quantise_wv(row_banks):
-            grouped = [turn_four(row_banks, [wv_words[:, 4 * f + r, :] for r in range(4)]) for f in range(2)]
-            for f in range(2):
-                quantise_four(grouped[f], wv_codes[:, f], wv_scales[:, f])
-
-        qk_turned, score, minus_a, minus_max, row_sum = {}, {}, {}, {}, {}
-        e_turned, e_codes, e_scales, v_grouped = {}, {}, {}, {}
-
-        def one_step(step, row_banks, e_banks, v_banks, o_banks):
-            def head(stage):
-                s = step - stage
-                return s if 0 <= s < HEADS else None
-
-            s = head(ATTEND)
-            if s is not None:
-                o_bank = o_banks.tile([P, TILES, DH], F32)
-                for n in range(TILES):
-                    nc.tensor.matmul_mx(
-                        out=o_bank[:, n, :],
-                        lhsT=e_codes[s][:, n * P : (n + 1) * P].bitcast(FP8X4),
-                        lhsT_scale=e_scales[s][:, n * P : (n + 1) * P],
-                        rhs=v_codes[:, s, :].bitcast(FP8X4),
-                        rhs_scale=v_scales[:, s, :],
-                        start=True,
-                        stop=True,
-                    )
-
-            s = head(ROW_MAX)
-            if s is not None:
-                nc.vector.tensor_tensor(
-                    out=minus_a[s][:],
-                    in0=penalty[:, s // H : s // H + 1, :].to_broadcast([P, TILES, S]),
-                    in1=minus_a[s][:],
-                    op=ALU.subtract,
-                )
-
-            s = head(ATTEND)
-            if s is not None:
-                inverse = pair.tile([P, TILES], F32)
-                nc.vector.reciprocal(out=inverse[:], in_=row_sum[s][:])
-                o = trio.tile([P, TILES, DH], F32)
-                nc.vector.tensor_tensor(
-                    out=o[:],
-                    in0=o_bank[:],
-                    in1=inverse[:].unsqueeze(2).to_broadcast([P, TILES, DH]),
-                    op=ALU.mult,
-                )
-                b, h = divmod(s, H)
-                nc.sync.dma_start(
-                    out=out[:, b, h * DH : (h + 1) * DH].rearrange("(p n) c -> p n c", n=TILES), in_=o[:]
-                )
-
+        def turn_qk(s):
+            qk_bank[s] = qk_banks.tile([P, 2 * TILES, P], BF16, name="qk_bank")
+            bank = qk_bank[s]
             for n in range(TILES):
-                tile_now = TILES * (step - TANH) + n
-                if 0 <= tile_now < HEADS * TILES:
-                    s = tile_now // TILES
-                    if n == 0:
-                        minus_a[s] = trio.tile([P, TILES, S], F32, name="minus_a")
-                    nc.scalar.activation(
-                        out=minus_a[s][:, n, :], in_=score[tile_now][:], func=ACT.Tanh, scale=1.0 / math.sqrt(DH)
-                    )
-                tile_next = tile_now + SCORE_BANKS
-                if 0 <= tile_next < HEADS * TILES:
-                    s, m = divmod(tile_next, TILES)
-                    score[tile_next] = score_banks.tile([P, S], F32, name="score")
-                    nc.tensor.matmul(
-                        out=score[tile_next][:],
-                        lhsT=qk_turned[s][:, m, :],
-                        rhs=qk_turned[s][:, TILES : 2 * TILES, :].rearrange("p n t -> p (n t)"),
-                        start=True,
-                        stop=True,
+                nc.tensor.transpose(bank[:, TILES + n, :], k_sb[:, s, n % 2, n // 2, :], ident_bf16[:])
+            for n in range(TILES):
+                nc.tensor.transpose(bank[:, n, :], q_sb[:, s, n, :], ident_bf16[:])
+
+        def copy_qk(s):
+            bank = qk_bank[s]
+            qk_turned[s] = trio.tile([P, 2 * TILES, P], BF16, name="qk_turned")
+            nc.vector.tensor_tensor(
+                out=qk_turned[s][:, TILES : 2 * TILES, :].rearrange("p n t -> p (n t)"),
+                in0=bank[:, TILES : 2 * TILES, :].rearrange("p n t -> p (n t)"),
+                in1=kept[:, s // H, :],
+                op=ALU.mult,
+            )
+            nc.vector.tensor_copy(out=qk_turned[s][:, 0:TILES, :], in_=bank[:, 0:TILES, :])
+
+        def make_score(j):
+            s, n = divmod(j, TILES)
+            score[j] = score_banks.tile([P, S], F32, name="score")
+            nc.tensor.matmul(
+                out=score[j][:],
+                lhsT=qk_turned[s][:, n, :],
+                rhs=qk_turned[s][:, TILES : 2 * TILES, :].rearrange("p n t -> p (n t)"),
+                start=True,
+                stop=True,
+            )
+
+        def tanh(j):
+            minus_a[j] = five.tile([P, S], F32, name="minus_a")
+            nc.scalar.activation(out=minus_a[j][:], in_=score[j][:], func=ACT.Tanh, scale=-1.0 / math.sqrt(DH))
+
+        def row_max(j):
+            s, n = divmod(j, TILES)
+            if n == 0:
+                minus_max[s] = eight.tile([P, TILES], F32, name="minus_max")
+            nc.vector.tensor_reduce(out=minus_max[s][:, n : n + 1], in_=minus_a[j][:], axis=AXIS.X, op=ALU.min)
+
+        def exp(j):
+            s, n = divmod(j, TILES)
+            if n == 0:
+                e[s] = five.tile([P, TILES * S], BF16, name="e")
+                row_sum[s] = eight.tile([P, TILES], F32, name="row_sum")
+            nc.scalar.activation(
+                out=e[s][:, n * S : (n + 1) * S],
+                in_=minus_a[j][:],
+                func=ACT.Exp,
+                scale=-1.0,
+                bias=minus_max[s][:, n : n + 1],
+                accum_out=row_sum[s][:, n : n + 1],
+            )
+            if n == TILES - 1:
+                masked_e[s] = eight.tile([P, TILES], F32, name="masked_e")
+                nc.scalar.activation(out=masked_e[s][:], in_=minus_max[s][:], func=ACT.Exp)
+
+        def turn_e(s, half):
+            e_words = e[s][:].bitcast(F32)
+            e_turned[s, half] = e_banks.tile([P, 2, 2, P], F32, name="e_turned")
+            for m in range(2):
+                for u in range(2):
+                    first = (2 * half + m) * (S // 2) + u * P
+                    nc.tensor.transpose(e_turned[s, half][:, u, m, :], e_words[:, first : first + P], ident_f32[:])
+
+        def copy_e(s, half):
+            if half == 0:
+                e_grouped[s] = pair.tile([P, S * 4], BF16, name="e_grouped", align_bytes=64)
+            words = e_grouped[s][:].bitcast(F32).rearrange("p (i u) -> p i u", u=2)
+            copy = nc.vector.tensor_copy if (2 * s + half) % 4 == 3 else nc.scalar.copy
+            copy(
+                out=words[:, 2 * P * half : 2 * P * (half + 1), :],
+                in_=e_turned[s, half][:].rearrange("p u m i -> p (m i) u"),
+            )
+
+        def quantise_e(s):
+            e_codes[s] = pair.tile([P, S], U32, name="e_codes", align_bytes=64)
+            e_scales[s] = pair.tile([P, S], U8, name="e_scales", align_bytes=64)
+            nc.vector.quantize_mx(out=e_codes[s][:].bitcast(FP8X4), scales=e_scales[s][:], in_=e_grouped[s][:])
+
+        def project_v(s):
+            b, h = divmod(s, H)
+            v_bank[s] = mixed_banks.tile([P, 4, DH], F32, name="mixed")
+            for i in range(4):
+                r = 2 * (i % 2) + i // 2
+                for g in range(PASSES):
+                    nc.tensor.matmul_mx(
+                        out=v_bank[s][:, i, :],
+                        lhsT=x_codes[:, b, r, g, :].bitcast(FP8X4),
+                        lhsT_scale=x_scales[:, b, r, g, :],
+                        rhs=wv_codes[:, h // 4, h % 4, g, :].bitcast(FP8X4),
+                        rhs_scale=wv_scales[:, h // 4, h % 4, g, :],
+                        start=(g == 0),
+                        stop=(g == PASSES - 1),
                     )
 
-            s = head(ROW_MAX)
-            if s is not None:
-                minus_max[s] = trio.tile([P, TILES], F32, name="minus_max")
-                nc.vector.tensor_reduce(out=minus_max[s][:], in_=minus_a[s][:], axis=AXIS.X, op=ALU.min)
+        def copy_v(s):
+            b = s // H
+            v_grouped[s] = pair.tile([P, DH * 4], BF16, name="v_grouped", align_bytes=64)
+            nc.vector.tensor_tensor(
+                out=v_grouped[s][:].rearrange("p (c i) -> p c i", i=4),
+                in0=v_bank[s][:].rearrange("p i c -> p c i"),
+                in1=kept_rows[:, b : b + 1, :].to_broadcast([P, DH, 4]),
+                op=ALU.mult,
+            )
 
-            s = head(TURN_QK)
-            if s is not None:
-                bank = qk_banks.tile([P, 2 * TILES, P], BF16)
-                for n in range(TILES):
-                    nc.tensor.transpose(bank[:, n, :], q_sb[:, s, n, :], ident_bf16[:])
-                for n in range(TILES):
-                    nc.tensor.transpose(bank[:, TILES + n, :], k_sb[:, s, n, :], ident_bf16[:])
-                qk_turned[s] = trio.tile([P, 2 * TILES, P], BF16, name="qk_turned")
-                nc.vector.tensor_copy(out=qk_turned[s][:], in_=bank[:])
+        def quantise_v(s):
+            nc.vector.quantize_mx(
+                out=v_codes[:, s, :].bitcast(FP8X4), scales=v_scales[:, s, :], in_=v_grouped[s][:]
+            )
 
-            s = head(QUANTISE)
-            if s is not None:
-                e_grouped = pair.tile([P, S * 4], BF16, align_bytes=64)
-                e_grouped_words = e_grouped[:].bitcast(F32).rearrange("p (i u) -> p i u", u=2)
-                for half in range(2):
-                    nc.scalar.copy(
-                        out=e_grouped_words[:, 2 * P * half : 2 * P * (half + 1), :],
-                        in_=e_turned[s, half][:].rearrange("p u m i -> p (m i) u"),
-                    )
-                e_codes[s] = pair.tile([P, S], U32, name="e_codes", align_bytes=64)
-                e_scales[s] = pair.tile([P, S], U8, name="e_scales", align_bytes=64)
-                nc.vector.quantize_mx(out=e_codes[s][:].bitcast(FP8X4), scales=e_scales[s][:], in_=e_grouped[:])
-                nc.vector.quantize_mx(
-                    out=v_codes[:, s, :].bitcast(FP8X4), scales=v_scales[:, s, :], in_=v_grouped[s][:]
+        def attend(s):
+            o_bank[s] = mixed_banks.tile([P, TILES, DH], F32, name="mixed")
+            for n in range(TILES):
+                nc.tensor.matmul_mx(
+                    out=o_bank[s][:, n, :],
+                    lhsT=e_codes[s][:, n * P : (n + 1) * P].bitcast(FP8X4),
+                    lhsT_scale=e_scales[s][:, n * P : (n + 1) * P],
+                    rhs=v_codes[:, s, :].bitcast(FP8X4),
+                    rhs_scale=v_scales[:, s, :],
+                    start=True,
+                    stop=True,
                 )
 
-            if step == ROWS_STEPS[0]:
-                quantise_x(row_banks)
-            if step == ROWS_STEPS[1]:
-                quantise_wv(row_banks)
+        inverse = {}
 
-            s = head(EXP)
-            if s is not None:
-                b, h = divmod(s, H)
-                v_bank = v_banks.tile([P, TILES, DH], F32)
-                for t in range(TILES):
-                    for g in range(PASSES):
-                        nc.tensor.matmul_mx(
-                            out=v_bank[:, t, :],
-                            lhsT=x_codes[:, b, t, g, :].bitcast(FP8X4),
-                            lhsT_scale=x_scales[:, b, t, g, :],
-                            rhs=wv_codes[:, h // 4, h % 4, g, :].bitcast(FP8X4),
-                            rhs_scale=wv_scales[:, h // 4, h % 4, g, :],
-                            start=(g == 0),
-                            stop=(g == PASSES - 1),
-                        )
-                e = pair.tile([P, TILES * S], BF16)
-                row_sum[s] = four.tile([P, TILES], F32, name="row_sum")
-                for n in range(TILES):
-                    nc.scalar.activation(
-                        out=e[:, n * S : (n + 1) * S],
-                        in_=minus_a[s][:, n, :],
-                        func=ACT.Exp,
-                        scale=-1.0,
-                        bias=minus_max[s][:, n : n + 1],
-                        accum_out=row_sum[s][:, n : n + 1],
-                    )
-                v_grouped[s] = pair.tile([P, DH * 4], BF16, name="v_grouped", align_bytes=64)
-                nc.scalar.copy(
-                    out=v_grouped[s][:].rearrange("p (c t) -> p c t", t=TILES),
-                    in_=v_bank[:].rearrange("p t c -> p c t"),
-                )
-                e_words = e[:].bitcast(F32)
-                for half in range(2):
-                    e_turned[s, half] = e_banks.tile([P, 2, 2, P], F32, name="e_turned")
-                    for u in range(2):
-                        for m in range(2):
-                            first = (2 * half + m) * (S // 2) + u * P
-                            nc.tensor.transpose(
-                                e_turned[s, half][:, u, m, :], e_words[:, first : first + P], ident_f32[:]
-                            )
+        def invert(s):
+            total = pair.tile([P, TILES], F32, name="total")
+            nc.vector.scalar_tensor_tensor(
+                out=total[:],
+                in0=masked_e[s][:],
+                scalar=minus_masked[:, s // H : s // H + 1],
+                in1=row_sum[s][:],
+                op0=ALU.mult,
+                op1=ALU.add,
+            )
+            inverse[s] = pair.tile([P, TILES], F32, name="inverse")
+            nc.vector.reciprocal(out=inverse[s][:], in_=total[:])
 
-        with tc.psum_pool(name="row_banks", bufs=4) as row_banks:
-            for step in range(EXP):
-                one_step(step, row_banks, None, None, None)
-        with ExitStack() as late:
-            e_banks = late.enter_context(tc.psum_pool(name="e_banks", bufs=2, reuse_waits="tile"))
-            v_banks = late.enter_context(tc.psum_pool(name="v_banks", bufs=1, reuse_waits="tile"))
-            o_banks = late.enter_context(tc.psum_pool(name="o_banks", bufs=1, reuse_waits="tile"))
-            for step in range(EXP, HEADS + ATTEND + 1):
-                one_step(step, None, e_banks, v_banks, o_banks)
+        def divide(s):
+            b, h = divmod(s, H)
+            o = trio.tile([P, TILES, DH], F32, name="o")
+            nc.vector.tensor_tensor(
+                out=o[:],
+                in0=o_bank[s][:],
+                in1=inverse[s][:].unsqueeze(2).to_broadcast([P, TILES, DH]),
+                op=ALU.mult,
+            )
+            nc.sync.dma_start(
+                out=out[:, b, h * DH : (h + 1) * DH].rearrange("(p n) c -> p n c", n=TILES), in_=o[:]
+            )
+
+        spread_mask(0)
+        turn_qk(0)
+        take_mask(0)
+        copy_qk(0)
+        for j in range(SCORE_AHEAD):
+            make_score(j)
+        turn_qk(1)
+        copy_qk(1)
+
+        for slot in range(SLOTS):
+            stage = {}
+            for s in range(HEADS):
+                stage[slot - HEADS_FROM - HEAD_STEP * s] = s
+            r = slot - ROWS_FROM
+            ahead = divmod(slot + TURN_AHEAD, TILES)
+            behind = divmod(slot + TURN_AHEAD - 1, TILES)
+
+            if slot < ALL_TILES:
+                tanh(slot)
+            if 0 <= slot - EXP_BEHIND < ALL_TILES:
+                exp(slot - EXP_BEHIND)
+            if 0 <= slot - MAX_BEHIND < ALL_TILES:
+                row_max(slot - MAX_BEHIND)
+            if 3 in stage:
+                quantise_e(stage[3])
+                invert(stage[3])
+            if 1 in stage:
+                quantise_v(stage[1])
+            if 5 <= r < 18 and r % 4 == 1:
+                quantise_rows((r - 5) // 4)
+            if behind[1] == 0 and 1 < behind[0] < HEADS:
+                copy_qk(behind[0])
+            if 0 in stage:
+                copy_v(stage[0])
+            if 4 in stage:
+                divide(stage[4])
+            if 1 in stage:
+                copy_e(stage[1], 0)
+            if 2 in stage:
+                copy_e(stage[2], 1)
+            if 0 <= r - 1 < 16:
+                copy_rows(r - 1)
+            if r == 17:
+                take_mask(1)
+                take_mask_rows(0)
+                take_mask_rows(1)
+            if r == 16:
+                spread_mask(1)
+            if 0 in stage:
+                turn_e(stage[0], 0)
+            if 1 in stage:
+                turn_e(stage[1], 1)
+            if 0 <= r < 16:
+                turn_rows(r)
+            if ahead[1] == 0 and 1 < ahead[0] < HEADS:
+                turn_qk(ahead[0])
+            if slot + SCORE_AHEAD < ALL_TILES:
+                make_score(slot + SCORE_AHEAD)
+            if -1 in stage:
+                project_v(stage[-1])
+            if 3 in stage:
+                attend(stage[3])

@@ -54,7 +54,6 @@ def tile_attention_pa_kernel(tc, q, k, x, wv, mask, out):
         x_rows = x.rearrange("(p r) b d -> p b r d", r=4)
         wv_sb = keep.tile([P, H, D], BF16)
         wv_rows = wv.rearrange("h c d -> c h d")
-        mask_sb = keep.tile([P, B * S], BF16)
         mask_rows = keep.tile([P, B, 4], BF16)
 
         def load_qk(first, count):
@@ -62,8 +61,7 @@ def tile_attention_pa_kernel(tc, q, k, x, wv, mask, out):
             nc.sync.dma_start(out=k_sb[:, heads], in_=k_rows[:, heads])
             nc.sync.dma_start(out=q_sb[:, heads], in_=q_rows[:, heads])
 
-        nc.vector.memset(mask_sb[:], 0.0)
-        nc.scalar.dma_start(out=mask_sb[0:1, :], in_=mask.rearrange("b t -> (b t)").unsqueeze(0))
+        nc.scalar.dma_start(out=mask_rows[:], in_=mask.rearrange("b (p r) -> p b r", r=4))
         load_qk(0, 1)
         load_qk(1, 1)
         load_qk(2, 1)
@@ -71,7 +69,6 @@ def tile_attention_pa_kernel(tc, q, k, x, wv, mask, out):
         nc.sync.dma_start(out=x_sb[:, 0, 2:4], in_=x_rows[:, 0, 2:4])
         load_qk(3, 1)
         nc.sync.dma_start(out=wv_sb[:, 0:4], in_=wv_rows[:, 0:4])
-        nc.sync.dma_start(out=mask_rows[:], in_=mask.rearrange("b (p r) -> p b r", r=4))
         load_qk(4, 2)
         nc.sync.dma_start(out=wv_sb[:, 4:8], in_=wv_rows[:, 4:8])
         load_qk(6, 2)
@@ -88,32 +85,40 @@ def tile_attention_pa_kernel(tc, q, k, x, wv, mask, out):
 
         kept = keep.tile([P, B, S], BF16)
         kept_rows = keep.tile([P, B, 4], F32)
-        any_left = keep.tile([P, B], F32)
+        keys_left = keep.tile([P, B], F32)
         none_left = keep.tile([P, B], F32)
         minus_masked = keep.tile([P, B], F32)
-
         mask_bank = {}
 
-        def spread_mask(b):
-            mask_bank[b] = mixed_banks.tile([P, S], F32, name="mixed")
+        def count_keys():
+            bank = mixed_banks.tile([P, B, 4], F32, name="mixed")
             nc.tensor.matmul(
-                out=mask_bank[b][:], lhsT=ones[:], rhs=mask_sb[:, b * S : (b + 1) * S], start=True, stop=True
+                out=bank[:].rearrange("p b r -> p (b r)"),
+                lhsT=ones[:],
+                rhs=mask_rows[:].rearrange("p b r -> p (b r)"),
+                start=True,
+                stop=True,
+            )
+            nc.vector.tensor_reduce(out=keys_left[:], in_=bank[:], axis=AXIS.X, op=ALU.add)
+            nc.vector.tensor_scalar(
+                out=none_left[:], in0=keys_left[:], scalar1=-1.0, scalar2=1.0, op0=ALU.mult, op1=ALU.add
             )
 
+        def spread_mask(b):
+            mask_bank[b] = mixed_banks.tile([P, 4, P], F32, name="mixed")
+            for r in range(4):
+                nc.tensor.matmul(
+                    out=mask_bank[b][:, r, :],
+                    lhsT=mask_rows[:, b, r : r + 1].to_broadcast([P, P]),
+                    rhs=ident_bf16[:],
+                    start=True,
+                    stop=True,
+                )
+
         def take_mask(b):
-            bank = mask_bank[b]
-            nc.vector.tensor_reduce(out=any_left[:, b : b + 1], in_=bank[:], axis=AXIS.X, op=ALU.max)
             nc.vector.tensor_scalar(
-                out=none_left[:, b : b + 1],
-                in0=any_left[:, b : b + 1],
-                scalar1=-1.0,
-                scalar2=1.0,
-                op0=ALU.mult,
-                op1=ALU.add,
-            )
-            nc.vector.tensor_scalar(
-                out=kept[:, b, :].rearrange("p (u z) -> p u z", u=2),
-                in0=bank[:].rearrange("p (z u) -> p u z", u=2),
+                out=kept[:, b, :].rearrange("p (u z e) -> p u z e", u=2, e=2),
+                in0=mask_bank[b][:].rearrange("p (e u) z -> p u z e", u=2),
                 scalar1=none_left[:, b : b + 1],
                 scalar2=-float(S),
                 op0=ALU.max,
@@ -159,7 +164,7 @@ def tile_attention_pa_kernel(tc, q, k, x, wv, mask, out):
             if r % 4 == 0:
                 grouped_rows[r // 4] = pair.tile([P, 4 * PASSES * P * 4], BF16, name="grouped", align_bytes=64)
             words = grouped_rows[r // 4][:].bitcast(F32).rearrange("p (r g c u) -> p r g c u", r=4, g=PASSES, u=2)
-            copy = nc.scalar.copy if r % 2 == 0 else nc.vector.tensor_copy
+            copy = nc.scalar.copy if r % 4 == 0 else nc.vector.tensor_copy
             copy(out=words[:, r % 4], in_=turned_rows[r][:].rearrange("p u g c -> p g c u"))
 
         def quantise_rows(group):
@@ -243,16 +248,22 @@ def tile_attention_pa_kernel(tc, q, k, x, wv, mask, out):
             if half == 0:
                 e_grouped[s] = pair.tile([P, S * 4], BF16, name="e_grouped", align_bytes=64)
             words = e_grouped[s][:].bitcast(F32).rearrange("p (i u) -> p i u", u=2)
-            copy = nc.vector.tensor_copy if (2 * s + half) % 4 == 3 else nc.scalar.copy
+            copy = nc.vector.tensor_copy if (2 * s + half) % 8 == 1 else nc.scalar.copy
             copy(
                 out=words[:, 2 * P * half : 2 * P * (half + 1), :],
                 in_=e_turned[s, half][:].rearrange("p u m i -> p (m i) u"),
             )
 
-        def quantise_e(s):
-            e_codes[s] = pair.tile([P, S], U32, name="e_codes", align_bytes=64)
-            e_scales[s] = pair.tile([P, S], U8, name="e_scales", align_bytes=64)
-            nc.vector.quantize_mx(out=e_codes[s][:].bitcast(FP8X4), scales=e_scales[s][:], in_=e_grouped[s][:])
+        def quantise_e(s, half):
+            if half == 0:
+                e_codes[s] = pair.tile([P, S], U32, name="e_codes", align_bytes=64)
+                e_scales[s] = pair.tile([P, S], U8, name="e_scales", align_bytes=64)
+            queries = slice(2 * P * half, 2 * P * (half + 1))
+            nc.vector.quantize_mx(
+                out=e_codes[s][:, queries].bitcast(FP8X4),
+                scales=e_scales[s][:, queries],
+                in_=e_grouped[s][:, 8 * P * half : 8 * P * (half + 1)],
+            )
 
         def project_v(s):
             b, h = divmod(s, H)
@@ -298,20 +309,24 @@ def tile_attention_pa_kernel(tc, q, k, x, wv, mask, out):
                     stop=True,
                 )
 
-        inverse = {}
+        total, inverse = {}, {}
 
-        def invert(s):
-            total = pair.tile([P, TILES], F32, name="total")
-            nc.vector.scalar_tensor_tensor(
-                out=total[:],
+        def add_up(s):
+            share = pair.tile([P, TILES], F32, name="share")
+            nc.gpsimd.tensor_scalar(
+                out=share[:],
                 in0=masked_e[s][:],
-                scalar=minus_masked[:, s // H : s // H + 1],
-                in1=row_sum[s][:],
+                scalar1=minus_masked[:, s // H : s // H + 1],
+                scalar2=0.0,
                 op0=ALU.mult,
                 op1=ALU.add,
             )
+            total[s] = eight.tile([P, TILES], F32, name="total")
+            nc.gpsimd.tensor_tensor(out=total[s][:], in0=share[:], in1=row_sum[s][:], op=ALU.add)
+
+        def invert(s):
             inverse[s] = pair.tile([P, TILES], F32, name="inverse")
-            nc.vector.reciprocal(out=inverse[s][:], in_=total[:])
+            nc.vector.reciprocal(out=inverse[s][:], in_=total[s][:])
 
         def divide(s):
             b, h = divmod(s, H)
@@ -326,6 +341,7 @@ def tile_attention_pa_kernel(tc, q, k, x, wv, mask, out):
                 out=out[:, b, h * DH : (h + 1) * DH].rearrange("(p n) c -> p n c", n=TILES), in_=o[:]
             )
 
+        count_keys()
         spread_mask(0)
         turn_qk(0)
         take_mask(0)
@@ -334,6 +350,7 @@ def tile_attention_pa_kernel(tc, q, k, x, wv, mask, out):
             make_score(j)
         turn_qk(1)
         copy_qk(1)
+        take_mask_rows(0)
 
         for slot in range(SLOTS):
             stage = {}
@@ -347,10 +364,14 @@ def tile_attention_pa_kernel(tc, q, k, x, wv, mask, out):
                 tanh(slot)
             if 0 <= slot - EXP_BEHIND < ALL_TILES:
                 exp(slot - EXP_BEHIND)
+                if (slot - EXP_BEHIND) % TILES == TILES - 1:
+                    add_up((slot - EXP_BEHIND) // TILES)
             if 0 <= slot - MAX_BEHIND < ALL_TILES:
                 row_max(slot - MAX_BEHIND)
+            if 2 in stage:
+                quantise_e(stage[2], 0)
             if 3 in stage:
-                quantise_e(stage[3])
+                quantise_e(stage[3], 1)
                 invert(stage[3])
             if 1 in stage:
                 quantise_v(stage[1])
@@ -370,7 +391,6 @@ def tile_attention_pa_kernel(tc, q, k, x, wv, mask, out):
                 copy_rows(r - 1)
             if r == 17:
                 take_mask(1)
-                take_mask_rows(0)
                 take_mask_rows(1)
             if r == 16:
                 spread_mask(1)

@@ -248,7 +248,7 @@ def tile_attention_pa_kernel(tc, q, k, x, wv, mask, out):
             if half == 0:
                 e_grouped[s] = pair.tile([P, S * 4], BF16, name="e_grouped", align_bytes=64)
             words = e_grouped[s][:].bitcast(F32).rearrange("p (i u) -> p i u", u=2)
-            copy = nc.vector.tensor_copy if (2 * s + half) % 8 == 1 else nc.scalar.copy
+            copy = nc.vector.tensor_copy if (2 * s + half) % 4 == 1 else nc.scalar.copy
             copy(
                 out=words[:, 2 * P * half : 2 * P * (half + 1), :],
                 in_=e_turned[s, half][:].rearrange("p u m i -> p (m i) u"),

@@ -30,6 +30,8 @@ HEAD_STEP = 3
 LAST_HEAD = ALL_TILES + 2
 HEADS_FROM = LAST_HEAD - HEAD_STEP * (HEADS - 1)
 SLOTS = LAST_HEAD + 6
+LAST = HEADS - 1
+LAST_PIECES = [(LAST, 0, 2), (LAST, 2, 1), (LAST, 3, 1)]
 
 
 def tile_attention_pa_kernel(tc, q, k, x, wv, mask, out):
@@ -39,7 +41,7 @@ def tile_attention_pa_kernel(tc, q, k, x, wv, mask, out):
         pair = stack.enter_context(tc.tile_pool(name="pair", bufs=2))
         trio = stack.enter_context(tc.tile_pool(name="trio", bufs=3))
         five = stack.enter_context(tc.tile_pool(name="five", bufs=5))
-        eight = stack.enter_context(tc.tile_pool(name="eight", bufs=8))
+        four = stack.enter_context(tc.tile_pool(name="four", bufs=4))
         score_banks = stack.enter_context(tc.psum_pool(name="score_banks", bufs=SCORE_AHEAD))
         qk_banks = stack.enter_context(tc.psum_pool(name="qk_banks", bufs=1))
         e_banks = stack.enter_context(tc.psum_pool(name="e_banks", bufs=2))
@@ -56,13 +58,13 @@ def tile_attention_pa_kernel(tc, q, k, x, wv, mask, out):
         wv_rows = wv.rearrange("h c d -> c h d")
         mask_rows = keep.tile([P, B, 4], BF16)
 
-        def load_qk(first, count):
+        def load_qk(first, count, q_queue=nc.sync):
             heads = slice(first, first + count)
             nc.sync.dma_start(out=k_sb[:, heads], in_=k_rows[:, heads])
-            nc.sync.dma_start(out=q_sb[:, heads], in_=q_rows[:, heads])
+            q_queue.dma_start(out=q_sb[:, heads], in_=q_rows[:, heads])
 
         nc.scalar.dma_start(out=mask_rows[:], in_=mask.rearrange("b (p r) -> p b r", r=4))
-        load_qk(0, 1)
+        load_qk(0, 1, nc.scalar)
         load_qk(1, 1)
         load_qk(2, 1)
         nc.sync.dma_start(out=x_sb[:, 0, 0:2], in_=x_rows[:, 0, 0:2])
@@ -78,6 +80,8 @@ def tile_attention_pa_kernel(tc, q, k, x, wv, mask, out):
 
         ones = keep.tile([P, P], BF16)
         nc.vector.memset(ones[:], 1.0)
+        zeros = keep.tile([P, S], BF16)
+        nc.vector.memset(zeros[:], 0.0)
         ident_bf16 = keep.tile([P, P], BF16)
         make_identity(nc, ident_bf16[:])
         ident_f32 = keep.tile([P, P], F32)
@@ -105,7 +109,7 @@ def tile_attention_pa_kernel(tc, q, k, x, wv, mask, out):
             )
 
         def spread_mask(b):
-            mask_bank[b] = mixed_banks.tile([P, 4, P], F32, name="mixed")
+            mask_bank[b] = e_banks.tile([P, 4, P], F32, name="e_turned")
             for r in range(4):
                 nc.tensor.matmul(
                     out=mask_bank[b][:, r, :],
@@ -164,7 +168,7 @@ def tile_attention_pa_kernel(tc, q, k, x, wv, mask, out):
             if r % 4 == 0:
                 grouped_rows[r // 4] = pair.tile([P, 4 * PASSES * P * 4], BF16, name="grouped", align_bytes=64)
             words = grouped_rows[r // 4][:].bitcast(F32).rearrange("p (r g c u) -> p r g c u", r=4, g=PASSES, u=2)
-            copy = nc.scalar.copy if r % 4 == 0 else nc.vector.tensor_copy
+            copy = nc.scalar.copy if r % 3 == 1 else nc.vector.tensor_copy
             copy(out=words[:, r % 4], in_=turned_rows[r][:].rearrange("p u g c -> p g c u"))
 
         def quantise_rows(group):
@@ -215,54 +219,59 @@ def tile_attention_pa_kernel(tc, q, k, x, wv, mask, out):
 
         def row_max(j):
             s, n = divmod(j, TILES)
-            if n == 0:
-                minus_max[s] = eight.tile([P, TILES], F32, name="minus_max")
-            nc.vector.tensor_reduce(out=minus_max[s][:, n : n + 1], in_=minus_a[j][:], axis=AXIS.X, op=ALU.min)
+            if n == 0 and s % 2 == 0:
+                minus_max[s // 2] = four.tile([P, 2 * TILES], F32, name="minus_max")
+            column = j % (2 * TILES)
+            nc.vector.tensor_reduce(out=minus_max[s // 2][:, column : column + 1], in_=minus_a[j][:], axis=AXIS.X, op=ALU.min)
 
         def exp(j):
             s, n = divmod(j, TILES)
             if n == 0:
                 e[s] = five.tile([P, TILES * S], BF16, name="e")
-                row_sum[s] = eight.tile([P, TILES], F32, name="row_sum")
+                if s % 2 == 0:
+                    row_sum[s // 2] = four.tile([P, 2 * TILES], F32, name="row_sum")
+            column = j % (2 * TILES)
             nc.scalar.activation(
                 out=e[s][:, n * S : (n + 1) * S],
                 in_=minus_a[j][:],
                 func=ACT.Exp,
                 scale=-1.0,
-                bias=minus_max[s][:, n : n + 1],
-                accum_out=row_sum[s][:, n : n + 1],
+                bias=minus_max[s // 2][:, column : column + 1],
+                accum_out=row_sum[s // 2][:, column : column + 1],
             )
-            if n == TILES - 1:
-                masked_e[s] = eight.tile([P, TILES], F32, name="masked_e")
-                nc.scalar.activation(out=masked_e[s][:], in_=minus_max[s][:], func=ACT.Exp)
+            if column == 2 * TILES - 1:
+                masked_e[s // 2] = four.tile([P, 2 * TILES], F32, name="masked_e")
+                nc.scalar.activation(out=masked_e[s // 2][:], in_=minus_max[s // 2][:], func=ACT.Exp)
 
-        def turn_e(s, half):
+        def turn_e(piece):
+            s, first, count = piece
             e_words = e[s][:].bitcast(F32)
-            e_turned[s, half] = e_banks.tile([P, 2, 2, P], F32, name="e_turned")
-            for m in range(2):
+            e_turned[piece] = e_banks.tile([P, 2, count, P], F32, name="e_turned")
+            for m in range(count):
                 for u in range(2):
-                    first = (2 * half + m) * (S // 2) + u * P
-                    nc.tensor.transpose(e_turned[s, half][:, u, m, :], e_words[:, first : first + P], ident_f32[:])
+                    word = (first + m) * (S // 2) + u * P
+                    nc.tensor.transpose(e_turned[piece][:, u, m, :], e_words[:, word : word + P], ident_f32[:])
 
-        def copy_e(s, half):
-            if half == 0:
+        def copy_e(piece, copy):
+            s, first, count = piece
+            if first == 0:
                 e_grouped[s] = pair.tile([P, S * 4], BF16, name="e_grouped", align_bytes=64)
             words = e_grouped[s][:].bitcast(F32).rearrange("p (i u) -> p i u", u=2)
-            copy = nc.vector.tensor_copy if (2 * s + half) % 4 == 1 else nc.scalar.copy
             copy(
-                out=words[:, 2 * P * half : 2 * P * (half + 1), :],
-                in_=e_turned[s, half][:].rearrange("p u m i -> p (m i) u"),
+                out=words[:, P * first : P * (first + count), :],
+                in_=e_turned[piece][:].rearrange("p u m i -> p (m i) u"),
             )
 
-        def quantise_e(s, half):
-            if half == 0:
+        def quantise_e(piece):
+            s, first, count = piece
+            if first == 0:
                 e_codes[s] = pair.tile([P, S], U32, name="e_codes", align_bytes=64)
                 e_scales[s] = pair.tile([P, S], U8, name="e_scales", align_bytes=64)
-            queries = slice(2 * P * half, 2 * P * (half + 1))
+            queries = slice(P * first, P * (first + count))
             nc.vector.quantize_mx(
                 out=e_codes[s][:, queries].bitcast(FP8X4),
                 scales=e_scales[s][:, queries],
-                in_=e_grouped[s][:, 8 * P * half : 8 * P * (half + 1)],
+                in_=e_grouped[s][:, 4 * P * first : 4 * P * (first + count)],
             )
 
         def project_v(s):
@@ -296,13 +305,15 @@ def tile_attention_pa_kernel(tc, q, k, x, wv, mask, out):
                 out=v_codes[:, s, :].bitcast(FP8X4), scales=v_scales[:, s, :], in_=v_grouped[s][:]
             )
 
-        def attend(s):
-            o_bank[s] = mixed_banks.tile([P, TILES, DH], F32, name="mixed")
-            for n in range(TILES):
+        def attend(piece):
+            s, first, count = piece
+            o_bank[piece] = mixed_banks.tile([P, count, DH], F32, name="mixed")
+            for m in range(count):
+                queries = slice(P * (first + m), P * (first + m + 1))
                 nc.tensor.matmul_mx(
-                    out=o_bank[s][:, n, :],
-                    lhsT=e_codes[s][:, n * P : (n + 1) * P].bitcast(FP8X4),
-                    lhsT_scale=e_scales[s][:, n * P : (n + 1) * P],
+                    out=o_bank[piece][:, m, :],
+                    lhsT=e_codes[s][:, queries].bitcast(FP8X4),
+                    lhsT_scale=e_scales[s][:, queries],
                     rhs=v_codes[:, s, :].bitcast(FP8X4),
                     rhs_scale=v_scales[:, s, :],
                     start=True,
@@ -311,36 +322,44 @@ def tile_attention_pa_kernel(tc, q, k, x, wv, mask, out):
 
         total, inverse = {}, {}
 
-        def add_up(s):
-            share = pair.tile([P, TILES], F32, name="share")
+        def add_up(two):
+            share = pair.tile([P, 2 * TILES], F32, name="share")
+            b = 2 * two // H
             nc.gpsimd.tensor_scalar(
                 out=share[:],
-                in0=masked_e[s][:],
-                scalar1=minus_masked[:, s // H : s // H + 1],
+                in0=masked_e[two][:],
+                scalar1=minus_masked[:, b : b + 1],
                 scalar2=0.0,
                 op0=ALU.mult,
                 op1=ALU.add,
             )
-            total[s] = eight.tile([P, TILES], F32, name="total")
-            nc.gpsimd.tensor_tensor(out=total[s][:], in0=share[:], in1=row_sum[s][:], op=ALU.add)
+            total[two] = four.tile([P, 2 * TILES], F32, name="total")
+            nc.gpsimd.tensor_tensor(out=total[two][:], in0=share[:], in1=row_sum[two][:], op=ALU.add)
 
-        def invert(s):
-            inverse[s] = pair.tile([P, TILES], F32, name="inverse")
-            nc.vector.reciprocal(out=inverse[s][:], in_=total[s][:])
+        def invert(two):
+            inverse[two] = pair.tile([P, 2 * TILES], F32, name="inverse")
+            nc.vector.reciprocal(out=inverse[two][:], in_=total[two][:])
 
-        def divide(s):
+        def divide(piece):
+            s, first, count = piece
             b, h = divmod(s, H)
-            o = trio.tile([P, TILES, DH], F32, name="o")
+            o = trio.tile([P, count, DH], F32, name="o")
+            column = TILES * (s % 2) + first
             nc.vector.tensor_tensor(
                 out=o[:],
-                in0=o_bank[s][:],
-                in1=inverse[s][:].unsqueeze(2).to_broadcast([P, TILES, DH]),
+                in0=o_bank[piece][:],
+                in1=inverse[s // 2][:, column : column + count].unsqueeze(2).to_broadcast([P, count, DH]),
                 op=ALU.mult,
             )
-            nc.sync.dma_start(
-                out=out[:, b, h * DH : (h + 1) * DH].rearrange("(p n) c -> p n c", n=TILES), in_=o[:]
-            )
+            rows = out[:, b, h * DH : (h + 1) * DH].rearrange("(p n) c -> p n c", n=TILES)
+            nc.sync.dma_start(out=rows[:, first : first + count, :], in_=o[:])
 
+        def warm_up():
+            bank = e_banks.tile([P, S], F32, name="e_turned")
+            for i in range(4):
+                nc.tensor.matmul(out=bank[:], lhsT=ones[:], rhs=zeros[:], start=True, stop=True)
+
+        warm_up()
         count_keys()
         spread_mask(0)
         turn_qk(0)
@@ -356,6 +375,7 @@ def tile_attention_pa_kernel(tc, q, k, x, wv, mask, out):
             stage = {}
             for s in range(HEADS):
                 stage[slot - HEADS_FROM - HEAD_STEP * s] = s
+            last = {slot - ALL_TILES - 1 - i: piece for i, piece in enumerate(LAST_PIECES)}
             r = slot - ROWS_FROM
             ahead = divmod(slot + TURN_AHEAD, TILES)
             behind = divmod(slot + TURN_AHEAD - 1, TILES)
@@ -364,15 +384,17 @@ def tile_attention_pa_kernel(tc, q, k, x, wv, mask, out):
                 tanh(slot)
             if 0 <= slot - EXP_BEHIND < ALL_TILES:
                 exp(slot - EXP_BEHIND)
-                if (slot - EXP_BEHIND) % TILES == TILES - 1:
-                    add_up((slot - EXP_BEHIND) // TILES)
+                two, column = divmod(slot - EXP_BEHIND, 2 * TILES)
+                if column == 2 * TILES - 1:
+                    add_up(two)
             if 0 <= slot - MAX_BEHIND < ALL_TILES:
                 row_max(slot - MAX_BEHIND)
-            if 2 in stage:
-                quantise_e(stage[2], 0)
-            if 3 in stage:
-                quantise_e(stage[3], 1)
-                invert(stage[3])
+            if 2 in stage and stage[2] != LAST:
+                quantise_e((stage[2], 0, 2))
+            if 3 in stage and stage[3] != LAST:
+                quantise_e((stage[3], 2, 2))
+            if 2 in last:
+                quantise_e(last[2])
             if 1 in stage:
                 quantise_v(stage[1])
             if 5 <= r < 18 and r % 4 == 1:
@@ -381,12 +403,20 @@ def tile_attention_pa_kernel(tc, q, k, x, wv, mask, out):
                 copy_qk(behind[0])
             if 0 in stage:
                 copy_v(stage[0])
-            if 4 in stage:
-                divide(stage[4])
-            if 1 in stage:
-                copy_e(stage[1], 0)
-            if 2 in stage:
-                copy_e(stage[2], 1)
+            if 4 in stage and stage[4] != LAST:
+                if stage[4] % 2 == 0:
+                    invert(stage[4] // 2)
+                divide((stage[4], 0, TILES))
+            if slot == ALL_TILES + 5:
+                divide((LAST, 0, 3))
+            if slot == ALL_TILES + 6:
+                divide((LAST, 3, 1))
+            if 1 in stage and stage[1] != LAST:
+                copy_e((stage[1], 0, 2), nc.scalar.copy)
+            if 1 in last:
+                copy_e(last[1], nc.scalar.copy)
+            if 2 in stage and stage[2] != LAST:
+                copy_e((stage[2], 2, 2), nc.scalar.copy if stage[2] % 2 == 1 or slot > ALL_TILES else nc.vector.tensor_copy)
             if 0 <= r - 1 < 16:
                 copy_rows(r - 1)
             if r == 17:
@@ -394,10 +424,12 @@ def tile_attention_pa_kernel(tc, q, k, x, wv, mask, out):
                 take_mask_rows(1)
             if r == 16:
                 spread_mask(1)
-            if 0 in stage:
-                turn_e(stage[0], 0)
-            if 1 in stage:
-                turn_e(stage[1], 1)
+            if 0 in stage and stage[0] != LAST:
+                turn_e((stage[0], 0, 2))
+            if 1 in stage and stage[1] != LAST:
+                turn_e((stage[1], 2, 2))
+            if 0 in last:
+                turn_e(last[0])
             if 0 <= r < 16:
                 turn_rows(r)
             if ahead[1] == 0 and 1 < ahead[0] < HEADS:
@@ -406,5 +438,9 @@ def tile_attention_pa_kernel(tc, q, k, x, wv, mask, out):
                 make_score(slot + SCORE_AHEAD)
             if -1 in stage:
                 project_v(stage[-1])
-            if 3 in stage:
-                attend(stage[3])
+            if 3 in stage and stage[3] != LAST:
+                attend((stage[3], 0, TILES))
+            if slot == ALL_TILES + 4:
+                attend((LAST, 0, 3))
+            if slot == ALL_TILES + 5:
+                attend((LAST, 3, 1))

@@ -25,7 +25,8 @@ SCORE_AHEAD = 3
 MAX_BEHIND = 1
 EXP_BEHIND = 3
 TURN_AHEAD = 6
-ROWS_FROM = 3
+ROWS_BEFORE = 1
+ROWS_FROM = 4
 HEAD_STEP = 3
 LAST_HEAD = ALL_TILES + 2
 HEADS_FROM = LAST_HEAD - HEAD_STEP * (HEADS - 1)
@@ -65,10 +66,11 @@ def tile_attention_pa_kernel(tc, q, k, x, wv, mask, out):
 
         nc.scalar.dma_start(out=mask_rows[:], in_=mask.rearrange("b (p r) -> p b r", r=4))
         load_qk(0, 1, nc.scalar)
+        for r in range(ROWS_BEFORE):
+            nc.sync.dma_start(out=x_sb[:, 0, r], in_=x_rows[:, 0, r])
         load_qk(1, 1)
         load_qk(2, 1)
-        nc.sync.dma_start(out=x_sb[:, 0, 0:2], in_=x_rows[:, 0, 0:2])
-        nc.sync.dma_start(out=x_sb[:, 0, 2:4], in_=x_rows[:, 0, 2:4])
+        nc.sync.dma_start(out=x_sb[:, 0, ROWS_BEFORE:4], in_=x_rows[:, 0, ROWS_BEFORE:4])
         load_qk(3, 1)
         nc.sync.dma_start(out=wv_sb[:, 0:4], in_=wv_rows[:, 0:4])
         load_qk(4, 2)
@@ -80,8 +82,6 @@ def tile_attention_pa_kernel(tc, q, k, x, wv, mask, out):
 
         ones = keep.tile([P, P], BF16)
         nc.vector.memset(ones[:], 1.0)
-        zeros = keep.tile([P, S], BF16)
-        nc.vector.memset(zeros[:], 0.0)
         ident_bf16 = keep.tile([P, P], BF16)
         make_identity(nc, ident_bf16[:])
         ident_f32 = keep.tile([P, P], F32)
@@ -158,7 +158,10 @@ def tile_attention_pa_kernel(tc, q, k, x, wv, mask, out):
 
         def turn_rows(r):
             block = groups[r // 4][0][r % 4]
-            turned_rows[r] = mixed_banks.tile([P, 2, PASSES, P], F32, name="mixed")
+            if r % 2 == 0:
+                turned_rows[r] = mixed_banks.tile([P, 2, PASSES, P], F32, name="mixed")
+            else:
+                turned_rows[r] = e_banks.tile([P, 2, PASSES, P], F32, name="e_turned")
             for g in range(PASSES):
                 for u in range(2):
                     first = 256 * g + 128 * u
@@ -168,7 +171,7 @@ def tile_attention_pa_kernel(tc, q, k, x, wv, mask, out):
             if r % 4 == 0:
                 grouped_rows[r // 4] = pair.tile([P, 4 * PASSES * P * 4], BF16, name="grouped", align_bytes=64)
             words = grouped_rows[r // 4][:].bitcast(F32).rearrange("p (r g c u) -> p r g c u", r=4, g=PASSES, u=2)
-            copy = nc.scalar.copy if r % 3 == 1 else nc.vector.tensor_copy
+            copy = nc.scalar.copy if r % 3 == 0 else nc.vector.tensor_copy
             copy(out=words[:, r % 4], in_=turned_rows[r][:].rearrange("p u g c -> p g c u"))
 
         def quantise_rows(group):
@@ -355,9 +358,9 @@ def tile_attention_pa_kernel(tc, q, k, x, wv, mask, out):
             nc.sync.dma_start(out=rows[:, first : first + count, :], in_=o[:])
 
         def warm_up():
-            bank = e_banks.tile([P, S], F32, name="e_turned")
-            for i in range(4):
-                nc.tensor.matmul(out=bank[:], lhsT=ones[:], rhs=zeros[:], start=True, stop=True)
+            bank = e_banks.tile([P, P], F32, name="e_turned")
+            for i in range(12):
+                nc.tensor.matmul(out=bank[:], lhsT=ones[:], rhs=ones[:], start=True, stop=True)
 
         warm_up()
         count_keys()
@@ -365,6 +368,9 @@ def tile_attention_pa_kernel(tc, q, k, x, wv, mask, out):
         turn_qk(0)
         take_mask(0)
         copy_qk(0)
+        for r in range(ROWS_BEFORE):
+            turn_rows(r)
+            copy_rows(r)
         for j in range(SCORE_AHEAD):
             make_score(j)
         turn_qk(1)
@@ -376,7 +382,7 @@ def tile_attention_pa_kernel(tc, q, k, x, wv, mask, out):
             for s in range(HEADS):
                 stage[slot - HEADS_FROM - HEAD_STEP * s] = s
             last = {slot - ALL_TILES - 1 - i: piece for i, piece in enumerate(LAST_PIECES)}
-            r = slot - ROWS_FROM
+            r = slot - ROWS_FROM + ROWS_BEFORE
             ahead = divmod(slot + TURN_AHEAD, TILES)
             behind = divmod(slot + TURN_AHEAD - 1, TILES)
 
@@ -387,6 +393,8 @@ def tile_attention_pa_kernel(tc, q, k, x, wv, mask, out):
                 two, column = divmod(slot - EXP_BEHIND, 2 * TILES)
                 if column == 2 * TILES - 1:
                     add_up(two)
+            if 4 in stage and stage[4] % 2 == 0:
+                invert(stage[4] // 2)
             if 0 <= slot - MAX_BEHIND < ALL_TILES:
                 row_max(slot - MAX_BEHIND)
             if 2 in stage and stage[2] != LAST:
@@ -404,8 +412,6 @@ def tile_attention_pa_kernel(tc, q, k, x, wv, mask, out):
             if 0 in stage:
                 copy_v(stage[0])
             if 4 in stage and stage[4] != LAST:
-                if stage[4] % 2 == 0:
-                    invert(stage[4] // 2)
                 divide((stage[4], 0, TILES))
             if slot == ALL_TILES + 5:
                 divide((LAST, 0, 3))
@@ -416,8 +422,8 @@ def tile_attention_pa_kernel(tc, q, k, x, wv, mask, out):
             if 1 in last:
                 copy_e(last[1], nc.scalar.copy)
             if 2 in stage and stage[2] != LAST:
-                copy_e((stage[2], 2, 2), nc.scalar.copy if stage[2] % 2 == 1 or slot > ALL_TILES else nc.vector.tensor_copy)
-            if 0 <= r - 1 < 16:
+                copy_e((stage[2], 2, 2), nc.scalar.copy if stage[2] % 2 == 1 else nc.vector.tensor_copy)
+            if ROWS_BEFORE <= r - 1 < 16:
                 copy_rows(r - 1)
             if r == 17:
                 take_mask(1)
@@ -430,7 +436,7 @@ def tile_attention_pa_kernel(tc, q, k, x, wv, mask, out):
                 turn_e((stage[1], 2, 2))
             if 0 in last:
                 turn_e(last[0])
-            if 0 <= r < 16:
+            if ROWS_BEFORE <= r < 16:
                 turn_rows(r)
             if ahead[1] == 0 and 1 < ahead[0] < HEADS:
                 turn_qk(ahead[0])

@@ -368,13 +368,13 @@ def tile_attention_pa_kernel(tc, q, k, x, wv, mask, out):
         turn_qk(0)
         take_mask(0)
         copy_qk(0)
-        for r in range(ROWS_BEFORE):
-            turn_rows(r)
-            copy_rows(r)
-        for j in range(SCORE_AHEAD):
-            make_score(j)
+        turn_rows(0)
+        copy_rows(0)
+        make_score(0)
+        make_score(1)
         turn_qk(1)
         copy_qk(1)
+        make_score(2)
         take_mask_rows(0)
 
         for slot in range(SLOTS):
@@ -397,10 +397,8 @@ def tile_attention_pa_kernel(tc, q, k, x, wv, mask, out):
                 invert(stage[4] // 2)
             if 0 <= slot - MAX_BEHIND < ALL_TILES:
                 row_max(slot - MAX_BEHIND)
-            if 2 in stage and stage[2] != LAST:
-                quantise_e((stage[2], 0, 2))
             if 3 in stage and stage[3] != LAST:
-                quantise_e((stage[3], 2, 2))
+                quantise_e((stage[3], 0, TILES))
             if 2 in last:
                 quantise_e(last[2])
             if 1 in stage:

@@ -82,6 +82,10 @@ def tile_attention_pa_kernel(tc, q, k, x, wv, mask, out):
 
         ones = keep.tile([P, P], BF16)
         nc.vector.memset(ones[:], 1.0)
+        minus_ones = keep.tile([P, P], BF16)
+        nc.vector.memset(minus_ones[:], -1.0)
+        one_128th = keep.tile([P, B], BF16)
+        nc.vector.memset(one_128th[:], 1.0 / P)
         ident_bf16 = keep.tile([P, P], BF16)
         make_identity(nc, ident_bf16[:])
         ident_f32 = keep.tile([P, P], F32)
@@ -89,24 +93,17 @@ def tile_attention_pa_kernel(tc, q, k, x, wv, mask, out):
 
         kept = keep.tile([P, B, S], BF16)
         kept_rows = keep.tile([P, B, 4], F32)
-        keys_left = keep.tile([P, B], F32)
-        none_left = keep.tile([P, B], F32)
         minus_masked = keep.tile([P, B], F32)
         mask_bank = {}
 
+        none_left = mixed_banks.tile([P, B], F32, name="mixed")
+
         def count_keys():
-            bank = mixed_banks.tile([P, B, 4], F32, name="mixed")
-            nc.tensor.matmul(
-                out=bank[:].rearrange("p b r -> p (b r)"),
-                lhsT=ones[:],
-                rhs=mask_rows[:].rearrange("p b r -> p (b r)"),
-                start=True,
-                stop=True,
-            )
-            nc.vector.tensor_reduce(out=keys_left[:], in_=bank[:], axis=AXIS.X, op=ALU.add)
-            nc.vector.tensor_scalar(
-                out=none_left[:], in0=keys_left[:], scalar1=-1.0, scalar2=1.0, op0=ALU.mult, op1=ALU.add
-            )
+            nc.tensor.matmul(out=none_left[:], lhsT=ones[:], rhs=one_128th[:], start=True, stop=False)
+            for r in range(4):
+                nc.tensor.matmul(
+                    out=none_left[:], lhsT=minus_ones[:], rhs=mask_rows[:, :, r], start=False, stop=(r == 3)
+                )
 
         def spread_mask(b):
             mask_bank[b] = e_banks.tile([P, 4, P], F32, name="e_turned")
@@ -184,34 +181,35 @@ def tile_attention_pa_kernel(tc, q, k, x, wv, mask, out):
 
         qk_turned, score, minus_a, minus_max, row_sum, masked_e = {}, {}, {}, {}, {}, {}
         e, e_turned, e_grouped, e_codes, e_scales = {}, {}, {}, {}, {}
-        qk_bank, v_bank, v_grouped, o_bank = {}, {}, {}, {}
+        q_bank, k_bank, v_bank, v_grouped, o_bank = {}, {}, {}, {}, {}
 
         def turn_qk(s):
-            qk_bank[s] = qk_banks.tile([P, 2 * TILES, P], BF16, name="qk_bank")
-            bank = qk_bank[s]
+            bank = qk_banks.tile([P, 2, TILES, P], BF16, name="qk_bank")
+            k_bank[s] = bank[:, 1]
+            q_bank[s] = e_banks.tile([P, TILES, P], BF16, name="e_turned")[:] if s == 0 else bank[:, 0]
             for n in range(TILES):
-                nc.tensor.transpose(bank[:, TILES + n, :], k_sb[:, s, n % 2, n // 2, :], ident_bf16[:])
+                nc.tensor.transpose(k_bank[s][:, n, :], k_sb[:, s, n % 2, n // 2, :], ident_bf16[:])
             for n in range(TILES):
-                nc.tensor.transpose(bank[:, n, :], q_sb[:, s, n, :], ident_bf16[:])
+                nc.tensor.transpose(q_bank[s][:, n, :], q_sb[:, s, n, :], ident_bf16[:])
 
         def copy_qk(s):
-            bank = qk_bank[s]
-            qk_turned[s] = trio.tile([P, 2 * TILES, P], BF16, name="qk_turned")
+            qk_turned[s] = trio.tile([P, 2, TILES, P], BF16, name="qk_turned")
             nc.vector.tensor_tensor(
-                out=qk_turned[s][:, TILES : 2 * TILES, :].rearrange("p n t -> p (n t)"),
-                in0=bank[:, TILES : 2 * TILES, :].rearrange("p n t -> p (n t)"),
+                out=qk_turned[s][:, 1].rearrange("p n t -> p (n t)"),
+                in0=k_bank[s].rearrange("p n t -> p (n t)"),
                 in1=kept[:, s // H, :],
                 op=ALU.mult,
             )
-            nc.vector.tensor_copy(out=qk_turned[s][:, 0:TILES, :], in_=bank[:, 0:TILES, :])
+            q_copy = nc.scalar.copy if s == 0 else nc.vector.tensor_copy
+            q_copy(out=qk_turned[s][:, 0], in_=q_bank[s])
 
         def make_score(j):
             s, n = divmod(j, TILES)
             score[j] = score_banks.tile([P, S], F32, name="score")
             nc.tensor.matmul(
                 out=score[j][:],
-                lhsT=qk_turned[s][:, n, :],
-                rhs=qk_turned[s][:, TILES : 2 * TILES, :].rearrange("p n t -> p (n t)"),
+                lhsT=qk_turned[s][:, 0, n, :],
+                rhs=qk_turned[s][:, 1].rearrange("p n t -> p (n t)"),
                 start=True,
                 stop=True,
             )
@@ -370,12 +368,15 @@ def tile_attention_pa_kernel(tc, q, k, x, wv, mask, out):
         copy_qk(0)
         turn_rows(0)
         copy_rows(0)
+        spread_mask(1)
+        take_mask(1)
         make_score(0)
         make_score(1)
         turn_qk(1)
         copy_qk(1)
         make_score(2)
-        take_mask_rows(0)
+        for b in range(B):
+            take_mask_rows(b)
 
         for slot in range(SLOTS):
             stage = {}
@@ -411,10 +412,10 @@ def tile_attention_pa_kernel(tc, q, k, x, wv, mask, out):
                 copy_v(stage[0])
             if 4 in stage and stage[4] != LAST:
                 divide((stage[4], 0, TILES))
-            if slot == ALL_TILES + 5:
-                divide((LAST, 0, 3))
+            if slot == ALL_TILES + 4:
+                divide((LAST, 0, 2))
             if slot == ALL_TILES + 6:
-                divide((LAST, 3, 1))
+                divide((LAST, 2, 2))
             if 1 in stage and stage[1] != LAST:
                 copy_e((stage[1], 0, 2), nc.scalar.copy)
             if 1 in last:
@@ -423,11 +424,6 @@ def tile_attention_pa_kernel(tc, q, k, x, wv, mask, out):
                 copy_e((stage[2], 2, 2), nc.scalar.copy if stage[2] % 2 == 1 else nc.vector.tensor_copy)
             if ROWS_BEFORE <= r - 1 < 16:
                 copy_rows(r - 1)
-            if r == 17:
-                take_mask(1)
-                take_mask_rows(1)
-            if r == 16:
-                spread_mask(1)
             if 0 in stage and stage[0] != LAST:
                 turn_e((stage[0], 0, 2))
             if 1 in stage and stage[1] != LAST:
@@ -444,7 +440,7 @@ def tile_attention_pa_kernel(tc, q, k, x, wv, mask, out):
                 project_v(stage[-1])
             if 3 in stage and stage[3] != LAST:
                 attend((stage[3], 0, TILES))
-            if slot == ALL_TILES + 4:
-                attend((LAST, 0, 3))
+            if slot == ALL_TILES + 3:
+                attend((LAST, 0, 2))
             if slot == ALL_TILES + 5:
-                attend((LAST, 3, 1))
+                attend((LAST, 2, 2))

import math
from contextlib import ExitStack

import concourse.mybir as mybir
from concourse.masks import make_identity

F32 = mybir.dt.float32
BF16 = mybir.dt.bfloat16
U32 = mybir.dt.uint32
U8 = mybir.dt.uint8
FP8X4 = mybir.dt.float8_e4m3fn_x4
ACT = mybir.ActivationFunctionType
ALU = mybir.AluOpType
AXIS = mybir.AxisListType

P = 128
S, B, D, H, DH = 512, 2, 1024, 8, 128
HEADS = B * H
TILES = S // P
ALL_TILES = HEADS * TILES
PASSES = D // 512
FLOPS = 2 * (S * B) * (H * DH) * D + 2 * 2 * HEADS * S * S * DH

SCORE_AHEAD = 3
MAX_BEHIND = 1
EXP_BEHIND = 3
TURN_AHEAD = 6
ROWS_BEFORE = 1
ROWS_FROM = 4
HEAD_STEP = 3
LAST_HEAD = ALL_TILES + 2
HEADS_FROM = LAST_HEAD - HEAD_STEP * (HEADS - 1)
SLOTS = LAST_HEAD + 6
LAST = HEADS - 1
LAST_PIECES = [(LAST, 0, 2), (LAST, 2, 1), (LAST, 3, 1)]


def tile_attention_pa_kernel(tc, q, k, x, wv, mask, out):
    nc = tc.nc
    with ExitStack() as stack:
        keep = stack.enter_context(tc.tile_pool(name="keep", bufs=1))
        pair = stack.enter_context(tc.tile_pool(name="pair", bufs=2))
        trio = stack.enter_context(tc.tile_pool(name="trio", bufs=3))
        five = stack.enter_context(tc.tile_pool(name="five", bufs=5))
        four = stack.enter_context(tc.tile_pool(name="four", bufs=4))
        score_banks = stack.enter_context(tc.psum_pool(name="score_banks", bufs=SCORE_AHEAD))
        qk_banks = stack.enter_context(tc.psum_pool(name="qk_banks", bufs=1))
        e_banks = stack.enter_context(tc.psum_pool(name="e_banks", bufs=2))
        mixed_banks = stack.enter_context(tc.psum_pool(name="mixed_banks", bufs=2))
        stack.enter_context(tc.manual_schedule())

        q_sb = keep.tile([P, HEADS, TILES, DH], BF16)
        k_sb = keep.tile([P, HEADS, 2, 2, DH], BF16)
        q_rows = q.rearrange("b h (p n) d -> p (b h) n d", n=TILES)
        k_rows = k.rearrange("b h (f p u) d -> p (b h) f u d", f=2, u=2)
        x_sb = keep.tile([P, B, 4, D], BF16)
        x_rows = x.rearrange("(p r) b d -> p b r d", r=4)
        wv_sb = keep.tile([P, H, D], BF16)
        wv_rows = wv.rearrange("h c d -> c h d")
        mask_rows = keep.tile([P, B, 4], BF16)

        def load_qk(first, count, q_queue=nc.sync):
            heads = slice(first, first + count)
            nc.sync.dma_start(out=k_sb[:, heads], in_=k_rows[:, heads])
            q_queue.dma_start(out=q_sb[:, heads], in_=q_rows[:, heads])

        nc.scalar.dma_start(out=mask_rows[:], in_=mask.rearrange("b (p r) -> p b r", r=4))
        load_qk(0, 1, nc.scalar)
        for r in range(ROWS_BEFORE):
            nc.sync.dma_start(out=x_sb[:, 0, r], in_=x_rows[:, 0, r])
        load_qk(1, 1)
        load_qk(2, 1)
        nc.sync.dma_start(out=x_sb[:, 0, ROWS_BEFORE:4], in_=x_rows[:, 0, ROWS_BEFORE:4])
        load_qk(3, 1)
        nc.sync.dma_start(out=wv_sb[:, 0:4], in_=wv_rows[:, 0:4])
        load_qk(4, 2)
        nc.sync.dma_start(out=wv_sb[:, 4:8], in_=wv_rows[:, 4:8])
        load_qk(6, 2)
        nc.sync.dma_start(out=x_sb[:, 1], in_=x_rows[:, 1])
        for first in range(8, HEADS, 2):
            load_qk(first, 2)

        ones = keep.tile([P, P], BF16)
        nc.vector.memset(ones[:], 1.0)
        minus_ones = keep.tile([P, P], BF16)
        nc.vector.memset(minus_ones[:], -1.0)
        one_128th = keep.tile([P, B], BF16)
        nc.vector.memset(one_128th[:], 1.0 / P)
        ident_bf16 = keep.tile([P, P], BF16)
        make_identity(nc, ident_bf16[:])
        ident_f32 = keep.tile([P, P], F32)
        make_identity(nc, ident_f32[:])

        kept = keep.tile([P, B, S], BF16)
        kept_rows = keep.tile([P, B, 4], F32)
        minus_masked = keep.tile([P, B], F32)
        mask_bank = {}

        none_left = mixed_banks.tile([P, B], F32, name="mixed")

        def count_keys():
            nc.tensor.matmul(out=none_left[:], lhsT=ones[:], rhs=one_128th[:], start=True, stop=False)
            for r in range(4):
                nc.tensor.matmul(
                    out=none_left[:], lhsT=minus_ones[:], rhs=mask_rows[:, :, r], start=False, stop=(r == 3)
                )

        def spread_mask(b):
            mask_bank[b] = e_banks.tile([P, 4, P], F32, name="e_turned")
            for r in range(4):
                nc.tensor.matmul(
                    out=mask_bank[b][:, r, :],
                    lhsT=mask_rows[:, b, r : r + 1].to_broadcast([P, P]),
                    rhs=ident_bf16[:],
                    start=True,
                    stop=True,
                )

        def take_mask(b):
            nc.vector.tensor_scalar(
                out=kept[:, b, :].rearrange("p (u z e) -> p u z e", u=2, e=2),
                in0=mask_bank[b][:].rearrange("p (e u) z -> p u z e", u=2),
                scalar1=none_left[:, b : b + 1],
                scalar2=-float(S),
                op0=ALU.max,
                op1=ALU.add,
                accum_out=minus_masked[:, b : b + 1],
            )

        def take_mask_rows(b):
            nc.vector.tensor_scalar(
                out=kept_rows[:, b, :].rearrange("p (u e) -> p u e", u=2),
                in0=mask_rows[:, b, :].rearrange("p (e u) -> p u e", u=2),
                scalar1=none_left[:, b : b + 1],
                scalar2=None,
                op0=ALU.max,
            )

        x_words = x_sb[:].bitcast(F32)
        wv_words = wv_sb[:].bitcast(F32)
        x_codes = keep.tile([P, B, 4, PASSES, P], U32, align_bytes=64)
        x_scales = keep.tile([P, B, 4, PASSES, P], U8, align_bytes=64)
        wv_codes = keep.tile([P, 2, 4, PASSES, DH], U32, align_bytes=64)
        wv_scales = keep.tile([P, 2, 4, PASSES, DH], U8, align_bytes=64)
        v_codes = keep.tile([P, HEADS, DH], U32, align_bytes=64)
        v_scales = keep.tile([P, HEADS, DH], U8, align_bytes=64)

        groups = [
            ([x_words[:, 0, r, :] for r in range(4)], x_codes[:, 0], x_scales[:, 0]),
            ([wv_words[:, r, :] for r in range(4)], wv_codes[:, 0], wv_scales[:, 0]),
            ([wv_words[:, 4 + r, :] for r in range(4)], wv_codes[:, 1], wv_scales[:, 1]),
            ([x_words[:, 1, r, :] for r in range(4)], x_codes[:, 1], x_scales[:, 1]),
        ]
        turned_rows, grouped_rows = {}, {}

        def turn_rows(r):
            block = groups[r // 4][0][r % 4]
            if r % 2 == 0:
                turned_rows[r] = mixed_banks.tile([P, 2, PASSES, P], F32, name="mixed")
            else:
                turned_rows[r] = e_banks.tile([P, 2, PASSES, P], F32, name="e_turned")
            for g in range(PASSES):
                for u in range(2):
                    first = 256 * g + 128 * u
                    nc.tensor.transpose(turned_rows[r][:, u, g, :], block[:, first : first + P], ident_f32[:])

        def copy_rows(r):
            if r % 4 == 0:
                grouped_rows[r // 4] = pair.tile([P, 4 * PASSES * P * 4], BF16, name="grouped", align_bytes=64)
            words = grouped_rows[r // 4][:].bitcast(F32).rearrange("p (r g c u) -> p r g c u", r=4, g=PASSES, u=2)
            copy = nc.scalar.copy if r % 3 == 0 else nc.vector.tensor_copy
            copy(out=words[:, r % 4], in_=turned_rows[r][:].rearrange("p u g c -> p g c u"))

        def quantise_rows(group):
            codes, scales = groups[group][1:]
            nc.vector.quantize_mx(
                out=codes.rearrange("p r g c -> p (r g c)").bitcast(FP8X4),
                scales=scales.rearrange("p r g c -> p (r g c)"),
                in_=grouped_rows[group][:],
            )

        qk_turned, score, minus_a, minus_max, row_sum, masked_e = {}, {}, {}, {}, {}, {}
        e, e_turned, e_grouped, e_codes, e_scales = {}, {}, {}, {}, {}
        q_bank, k_bank, v_bank, v_grouped, o_bank = {}, {}, {}, {}, {}

        def turn_qk(s):
            bank = qk_banks.tile([P, 2, TILES, P], BF16, name="qk_bank")
            k_bank[s] = bank[:, 1]
            q_bank[s] = e_banks.tile([P, TILES, P], BF16, name="e_turned")[:] if s == 0 else bank[:, 0]
            for n in range(TILES):
                nc.tensor.transpose(k_bank[s][:, n, :], k_sb[:, s, n % 2, n // 2, :], ident_bf16[:])
            for n in range(TILES):
                nc.tensor.transpose(q_bank[s][:, n, :], q_sb[:, s, n, :], ident_bf16[:])

        def copy_qk(s):
            qk_turned[s] = trio.tile([P, 2, TILES, P], BF16, name="qk_turned")
            nc.vector.tensor_tensor(
                out=qk_turned[s][:, 1].rearrange("p n t -> p (n t)"),
                in0=k_bank[s].rearrange("p n t -> p (n t)"),
                in1=kept[:, s // H, :],
                op=ALU.mult,
            )
            q_copy = nc.scalar.copy if s == 0 else nc.vector.tensor_copy
            q_copy(out=qk_turned[s][:, 0], in_=q_bank[s])

        def make_score(j):
            s, n = divmod(j, TILES)
            score[j] = score_banks.tile([P, S], F32, name="score")
            nc.tensor.matmul(
                out=score[j][:],
                lhsT=qk_turned[s][:, 0, n, :],
                rhs=qk_turned[s][:, 1].rearrange("p n t -> p (n t)"),
                start=True,
                stop=True,
            )

        def tanh(j):
            minus_a[j] = five.tile([P, S], F32, name="minus_a")
            nc.scalar.activation(out=minus_a[j][:], in_=score[j][:], func=ACT.Tanh, scale=-1.0 / math.sqrt(DH))

        def row_max(j):
            s, n = divmod(j, TILES)
            if n == 0 and s % 2 == 0:
                minus_max[s // 2] = four.tile([P, 2 * TILES], F32, name="minus_max")
            column = j % (2 * TILES)
            nc.vector.tensor_reduce(out=minus_max[s // 2][:, column : column + 1], in_=minus_a[j][:], axis=AXIS.X, op=ALU.min)

        def exp(j):
            s, n = divmod(j, TILES)
            if n == 0:
                e[s] = five.tile([P, TILES * S], BF16, name="e")
                if s % 2 == 0:
                    row_sum[s // 2] = four.tile([P, 2 * TILES], F32, name="row_sum")
            column = j % (2 * TILES)
            nc.scalar.activation(
                out=e[s][:, n * S : (n + 1) * S],
                in_=minus_a[j][:],
                func=ACT.Exp,
                scale=-1.0,
                bias=minus_max[s // 2][:, column : column + 1],
                accum_out=row_sum[s // 2][:, column : column + 1],
            )
            if column == 2 * TILES - 1:
                masked_e[s // 2] = four.tile([P, 2 * TILES], F32, name="masked_e")
                nc.scalar.activation(out=masked_e[s // 2][:], in_=minus_max[s // 2][:], func=ACT.Exp)

        def turn_e(piece):
            s, first, count = piece
            e_words = e[s][:].bitcast(F32)
            e_turned[piece] = e_banks.tile([P, 2, count, P], F32, name="e_turned")
            for m in range(count):
                for u in range(2):
                    word = (first + m) * (S // 2) + u * P
                    nc.tensor.transpose(e_turned[piece][:, u, m, :], e_words[:, word : word + P], ident_f32[:])

        def copy_e(piece, copy):
            s, first, count = piece
            if first == 0:
                e_grouped[s] = pair.tile([P, S * 4], BF16, name="e_grouped", align_bytes=64)
            words = e_grouped[s][:].bitcast(F32).rearrange("p (i u) -> p i u", u=2)
            copy(
                out=words[:, P * first : P * (first + count), :],
                in_=e_turned[piece][:].rearrange("p u m i -> p (m i) u"),
            )

        def quantise_e(piece):
            s, first, count = piece
            if first == 0:
                e_codes[s] = pair.tile([P, S], U32, name="e_codes", align_bytes=64)
                e_scales[s] = pair.tile([P, S], U8, name="e_scales", align_bytes=64)
            queries = slice(P * first, P * (first + count))
            nc.vector.quantize_mx(
                out=e_codes[s][:, queries].bitcast(FP8X4),
                scales=e_scales[s][:, queries],
                in_=e_grouped[s][:, 4 * P * first : 4 * P * (first + count)],
            )

        def project_v(s):
            b, h = divmod(s, H)
            v_bank[s] = mixed_banks.tile([P, 4, DH], F32, name="mixed")
            for i in range(4):
                r = 2 * (i % 2) + i // 2
                for g in range(PASSES):
                    nc.tensor.matmul_mx(
                        out=v_bank[s][:, i, :],
                        lhsT=x_codes[:, b, r, g, :].bitcast(FP8X4),
                        lhsT_scale=x_scales[:, b, r, g, :],
                        rhs=wv_codes[:, h // 4, h % 4, g, :].bitcast(FP8X4),
                        rhs_scale=wv_scales[:, h // 4, h % 4, g, :],
                        start=(g == 0),
                        stop=(g == PASSES - 1),
                    )

        def copy_v(s):
            b = s // H
            v_grouped[s] = pair.tile([P, DH * 4], BF16, name="v_grouped", align_bytes=64)
            nc.vector.tensor_tensor(
                out=v_grouped[s][:].rearrange("p (c i) -> p c i", i=4),
                in0=v_bank[s][:].rearrange("p i c -> p c i"),
                in1=kept_rows[:, b : b + 1, :].to_broadcast([P, DH, 4]),
                op=ALU.mult,
            )

        def quantise_v(s):
            nc.vector.quantize_mx(
                out=v_codes[:, s, :].bitcast(FP8X4), scales=v_scales[:, s, :], in_=v_grouped[s][:]
            )

        def attend(piece):
            s, first, count = piece
            o_bank[piece] = mixed_banks.tile([P, count, DH], F32, name="mixed")
            for m in range(count):
                queries = slice(P * (first + m), P * (first + m + 1))
                nc.tensor.matmul_mx(
                    out=o_bank[piece][:, m, :],
                    lhsT=e_codes[s][:, queries].bitcast(FP8X4),
                    lhsT_scale=e_scales[s][:, queries],
                    rhs=v_codes[:, s, :].bitcast(FP8X4),
                    rhs_scale=v_scales[:, s, :],
                    start=True,
                    stop=True,
                )

        total, inverse = {}, {}

        def add_up(two):
            share = pair.tile([P, 2 * TILES], F32, name="share")
            b = 2 * two // H
            nc.gpsimd.tensor_scalar(
                out=share[:],
                in0=masked_e[two][:],
                scalar1=minus_masked[:, b : b + 1],
                scalar2=0.0,
                op0=ALU.mult,
                op1=ALU.add,
            )
            total[two] = four.tile([P, 2 * TILES], F32, name="total")
            nc.gpsimd.tensor_tensor(out=total[two][:], in0=share[:], in1=row_sum[two][:], op=ALU.add)

        def invert(two):
            inverse[two] = pair.tile([P, 2 * TILES], F32, name="inverse")
            nc.vector.reciprocal(out=inverse[two][:], in_=total[two][:])

        def divide(piece):
            s, first, count = piece
            b, h = divmod(s, H)
            o = trio.tile([P, count, DH], F32, name="o")
            column = TILES * (s % 2) + first
            nc.vector.tensor_tensor(
                out=o[:],
                in0=o_bank[piece][:],
                in1=inverse[s // 2][:, column : column + count].unsqueeze(2).to_broadcast([P, count, DH]),
                op=ALU.mult,
            )
            rows = out[:, b, h * DH : (h + 1) * DH].rearrange("(p n) c -> p n c", n=TILES)
            nc.sync.dma_start(out=rows[:, first : first + count, :], in_=o[:])

        def warm_up():
            bank = e_banks.tile([P, P], F32, name="e_turned")
            for i in range(12):
                nc.tensor.matmul(out=bank[:], lhsT=ones[:], rhs=ones[:], start=True, stop=True)

        warm_up()
        count_keys()
        spread_mask(0)
        turn_qk(0)
        take_mask(0)
        copy_qk(0)
        turn_rows(0)
        copy_rows(0)
        spread_mask(1)
        take_mask(1)
        make_score(0)
        make_score(1)
        turn_qk(1)
        copy_qk(1)
        make_score(2)
        for b in range(B):
            take_mask_rows(b)

        for slot in range(SLOTS):
            stage = {}
            for s in range(HEADS):
                stage[slot - HEADS_FROM - HEAD_STEP * s] = s
            last = {slot - ALL_TILES - 1 - i: piece for i, piece in enumerate(LAST_PIECES)}
            r = slot - ROWS_FROM + ROWS_BEFORE
            ahead = divmod(slot + TURN_AHEAD, TILES)
            behind = divmod(slot + TURN_AHEAD - 1, TILES)

            if slot < ALL_TILES:
                tanh(slot)
            if 0 <= slot - EXP_BEHIND < ALL_TILES:
                exp(slot - EXP_BEHIND)
                two, column = divmod(slot - EXP_BEHIND, 2 * TILES)
                if column == 2 * TILES - 1:
                    add_up(two)
            if 4 in stage and stage[4] % 2 == 0:
                invert(stage[4] // 2)
            if 0 <= slot - MAX_BEHIND < ALL_TILES:
                row_max(slot - MAX_BEHIND)
            if 3 in stage and stage[3] != LAST:
                quantise_e((stage[3], 0, TILES))
            if 2 in last:
                quantise_e(last[2])
            if 1 in stage:
                quantise_v(stage[1])
            if 5 <= r < 18 and r % 4 == 1:
                quantise_rows((r - 5) // 4)
            if behind[1] == 0 and 1 < behind[0] < HEADS:
                copy_qk(behind[0])
            if 0 in stage:
                copy_v(stage[0])
            if 4 in stage and stage[4] != LAST:
                divide((stage[4], 0, TILES))
            if slot == ALL_TILES + 4:
                divide((LAST, 0, 2))
            if slot == ALL_TILES + 6:
                divide((LAST, 2, 2))
            if 1 in stage and stage[1] != LAST:
                copy_e((stage[1], 0, 2), nc.scalar.copy)
            if 1 in last:
                copy_e(last[1], nc.scalar.copy)
            if 2 in stage and stage[2] != LAST:
                copy_e((stage[2], 2, 2), nc.scalar.copy if stage[2] % 2 == 1 else nc.vector.tensor_copy)
            if ROWS_BEFORE <= r - 1 < 16:
                copy_rows(r - 1)
            if 0 in stage and stage[0] != LAST:
                turn_e((stage[0], 0, 2))
            if 1 in stage and stage[1] != LAST:
                turn_e((stage[1], 2, 2))
            if 0 in last:
                turn_e(last[0])
            if ROWS_BEFORE <= r < 16:
                turn_rows(r)
            if ahead[1] == 0 and 1 < ahead[0] < HEADS:
                turn_qk(ahead[0])
            if slot + SCORE_AHEAD < ALL_TILES:
                make_score(slot + SCORE_AHEAD)
            if -1 in stage:
                project_v(stage[-1])
            if 3 in stage and stage[3] != LAST:
                attend((stage[3], 0, TILES))
            if slot == ALL_TILES + 3:
                attend((LAST, 0, 2))
            if slot == ALL_TILES + 5:
                attend((LAST, 2, 2))
